import numpy as np
import ml_dtypes


def mxq(x, axis, fmt="e4m3"):
    dtype, down = {"e4m3": (ml_dtypes.float8_e4m3fn, 7), "e5m2": (ml_dtypes.float8_e5m2, 14)}[fmt]
    v = np.moveaxis(np.asarray(x, np.float32).astype(ml_dtypes.bfloat16).astype(np.float64), axis, -1)
    blocks = v.reshape(v.shape[:-1] + (-1, 32))
    amax = np.abs(blocks).max(-1, keepdims=True)
    byte = np.maximum(np.where(amax > 0, np.frexp(amax)[1] - 1 + 127, 0) - down, 1)
    scale = np.exp2(byte - 127.0)
    codes = (blocks / scale).astype(np.float32).astype(dtype).astype(np.float64)
    return np.moveaxis((codes * scale).reshape(v.shape), -1, axis)


WIDE = False


def mx_kscale(k):
    if not WIDE:
        return np.ones(k)
    levels = np.array([10, -10, 5, -5, 0])
    a = np.random.permutation(np.resize(levels, k // 512 * 4)).reshape(k // 512, 4)
    idx = np.arange(k)
    return np.exp2(a[idx // 512, idx % 128 // 32])


BF16 = ml_dtypes.bfloat16


def bf(x):
    return np.asarray(x, np.float32).astype(BF16)


def f64(x):
    return np.asarray(x).astype(np.float64)


E2M1 = np.array([0.0, 0.5, 1.0, 1.5, 2.0, 3.0, 4.0, 6.0, -0.0, -0.5, -1.0, -1.5, -2.0, -3.0, -4.0, -6.0])


def pack_weight(w, fmt):
    k, n = w.shape
    w = f64(bf(w)).reshape(k // 32, 32, n)
    amax = np.abs(w).max(1)
    if fmt == "e4m3":
        byte = np.frexp(amax)[1] - 1 + 127 - 7
    else:
        mant, ex = np.frexp(amax / 6.0)
        byte = np.where(mant > 0.5, ex, ex - 1) + 127
    byte = np.clip(np.where(amax > 0, byte, 1), 1, 254)
    scaled = (w * np.exp2(127.0 - byte)[:, None, :]).reshape(k, n).astype(np.float32)
    by_word = np.ascontiguousarray(scaled.reshape(k // 512, 128, 4, n).transpose(0, 1, 3, 2))
    if fmt == "e4m3":
        words = by_word.astype(ml_dtypes.float8_e4m3fn).view(np.uint8)
    else:
        c = by_word.astype(ml_dtypes.float4_e2m1fn).view(np.uint8) & 0xF
        words = c[..., 0::2] | (c[..., 1::2] << 4)
    return np.ascontiguousarray(words), np.ascontiguousarray(byte.astype(np.uint8).reshape(k // 512, 16, n))


def unpack_weight(words, scales, fmt):
    g, p, n, _ = words.shape
    if fmt == "e4m3":
        vals = np.ascontiguousarray(words).view(ml_dtypes.float8_e4m3fn).astype(np.float64)
    else:
        nib = np.empty((g, p, n, 4), np.uint8)
        nib[..., 0::2] = words & 0xF
        nib[..., 1::2] = words >> 4
        vals = E2M1[nib]
    vals = vals * np.repeat(np.exp2(scales.astype(np.float64) - 127.0), 8, axis=1)[..., None]
    return vals.transpose(0, 1, 3, 2).reshape(g * 512, n)


B, S, D, F1, F2, F3, F4 = 512, 16, 256, 512, 128, 1024, 512
K = D + D


def setup_inputs():
    s, t = mx_kscale(K), mx_kscale(F1)
    x1 = bf(np.random.standard_normal((B, S, D)) * s[:D])
    x2 = bf(np.random.standard_normal((B, S, D)) * s[D:])
    W1 = np.random.standard_normal((S, K, F1)) * 1.0 / np.sqrt(K) / s[None, :, None] * t[None, None, :]
    b1 = bf(np.random.standard_normal((S, F1)) * 0.3 * t)
    W2 = np.random.standard_normal((S, F1, F2)) * 1.4 / np.sqrt(F1) / t[None, :, None]
    b2 = bf(np.random.standard_normal((S, F2)) * 0.3)
    W1_words, W1_scales = pack_weight(W1.reshape(-1, F1), "e4m3")
    W2_words, W2_scales = pack_weight(W2.reshape(-1, F2), "e4m3")
    return {"x1": x1,
            "x2": x2,
            "W1_words": W1_words,
            "W1_scales": W1_scales,
            "b1": b1,
            "W2_words": W2_words,
            "W2_scales": W2_scales,
            "b2": b2}


def reference(x1, x2, W1_words, W1_scales, b1, W2_words, W2_scales, b2):
    x = np.concatenate([f64(x1), f64(x2)], axis=-1).transpose(1, 0, 2)
    h = np.maximum((mxq(x, 2, "e4m3") @ unpack_weight(W1_words, W1_scales, "e4m3").reshape(S, K, F1)) + f64(b1)[:, None, :], 0.0)
    y = (mxq(h, 2, "e4m3") @ unpack_weight(W2_words, W2_scales, "e4m3").reshape(S, F1, F2)) + f64(b2)[:, None, :]
    return y.transpose(1, 0, 2)

@@ -1,0 +1,292 @@
+from contextlib import ExitStack
+
+import concourse.mybir as mybir
+from concourse.masks import make_identity
+
+F32 = mybir.dt.float32
+BF16 = mybir.dt.bfloat16
+I32 = mybir.dt.int32
+U32 = mybir.dt.uint32
+U8 = mybir.dt.uint8
+FP8X4 = mybir.dt.float8_e4m3fn_x4
+ADD = mybir.AluOpType.add
+RELU = mybir.ActivationFunctionType.Relu
+
+P = 128
+B = 512
+STYLES = 16
+D = 256
+K = 2 * D
+F1 = 512
+F2 = 128
+ROUND = 4
+ROUNDS = STYLES // ROUND
+BLOCKS = B // P
+UNIT_BLOCKS = 2
+UNIT_B = UNIT_BLOCKS * P
+HALVES = BLOCKS // UNIT_BLOCKS
+UNITS = STYLES * HALVES
+ROUND_UNITS = ROUND * HALVES
+LAST_LAG = 5
+QUADRANTS = 4
+
+FLOPS = 2 * STYLES * B * (K * F1 + F1 * F2)
+
+
+def tile_simplefusionmodule_pa_t_e_kernel(
+    tc, x1, x2, W1_words, W1_scales, b1, W2_words, W2_scales, b2, out
+):
+    nc = tc.nc
+    with ExitStack() as stack:
+        stack.enter_context(tc.manual_schedule())
+        keep = stack.enter_context(tc.tile_pool(name="keep", bufs=1))
+        work = stack.enter_context(tc.tile_pool(name="work", bufs=3))
+        psum_xt = stack.enter_context(tc.psum_pool(name="psum_xt", bufs=2))
+        psum_ht = stack.enter_context(tc.psum_pool(name="psum_ht", bufs=2))
+        psum_wide = stack.enter_context(tc.psum_pool(name="psum_wide", bufs=3))
+        psum_y = stack.enter_context(tc.psum_pool(name="psum_y", bufs=1))
+
+        x_all = keep.tile([P, ROUNDS, BLOCKS, ROUND, K], BF16)
+        w1_all = keep.tile([P, STYLES, F1], U32, align_bytes=64)
+        w2_all = keep.tile([P, STYLES, F2], U32, align_bytes=64)
+        w1_planes = keep.tile([P, STYLES, F1], U8, align_bytes=64)
+        w2_planes = keep.tile([P, STYLES, F2], U8, align_bytes=64)
+        b1_rows = keep.tile([P, F1], BF16)
+        b1_sorted = keep.tile([P, F1], BF16)
+        b2_rows = keep.tile([P, ROUND * F2], BF16)
+        b1_all = keep.tile([P, STYLES, F1], BF16)
+        b2_all = keep.tile([P, STYLES, F2], BF16)
+        ident_f32 = keep.tile([P, P], F32)
+        ident_bf16 = keep.tile([P, P], BF16)
+
+        nc.vector.memset(b1_rows[:], 0.0)
+        nc.vector.memset(b2_rows[:], 0.0)
+        nc.vector.memset(w1_planes[:].rearrange("p s n -> p (s n)").bitcast(I32), 0)
+        nc.vector.memset(w2_planes[:].rearrange("p s n -> p (s n)").bitcast(I32), 0)
+        make_identity(nc, ident_f32[:])
+        make_identity(nc, ident_bf16[:])
+
+        nc.scalar.dma_start(out=b1_rows[0:STYLES, :], in_=b1)
+        nc.scalar.dma_start(
+            out=b2_rows[0:ROUNDS, :], in_=b2.rearrange("(r a) f -> r (a f)", a=ROUND)
+        )
+
+        def load_x(r, block):
+            rows = slice(block * P, (block + 1) * P)
+            styles = slice(r * ROUND, (r + 1) * ROUND)
+            nc.sync.dma_start(out=x_all[:, r, block, :, 0:D], in_=x1[rows, styles, :])
+            nc.sync.dma_start(out=x_all[:, r, block, :, D:K], in_=x2[rows, styles, :])
+
+        def load_scales(planes, scales):
+            for quadrant in range(QUADRANTS):
+                nc.sync.dma_start(
+                    out=planes[32 * quadrant : 32 * quadrant + 4, :, :].bitcast(I32),
+                    in_=scales[:, 4 * quadrant : 4 * quadrant + 4, :]
+                    .rearrange("s q n -> q s n")
+                    .bitcast(I32),
+                )
+
+        def load_words(words_all, words, s):
+            nc.sync.dma_start(
+                out=words_all[:, s, :].bitcast(I32),
+                in_=words[s].rearrange("p n t -> p (n t)").bitcast(I32),
+            )
+
+        for r in range(ROUNDS):
+            load_x(r, 0)
+            load_x(r, 1)
+            if r == 0:
+                load_scales(w1_planes, W1_scales)
+            for a in range(ROUND):
+                load_words(w1_all, W1_words, r * ROUND + a)
+            if r == 0:
+                load_scales(w2_planes, W2_scales)
+            for a in range(ROUND):
+                load_words(w2_all, W2_words, r * ROUND + a)
+            load_x(r, 2)
+            load_x(r, 3)
+
+        nc.vector.tensor_copy(
+            out=b1_sorted[:].rearrange("s (u p e) -> s u p e", u=2, e=2),
+            in_=b1_rows[:].rearrange("s (p u e) -> s u p e", u=2, e=2),
+        )
+
+        def spread_biases(r):
+            for pair in range(ROUND // 2):
+                first = r * ROUND + 2 * pair
+                spread = psum_wide.tile([P, 2, F1], BF16, tag="wide")
+                for i in range(2):
+                    nc.tensor.matmul(
+                        out=spread[:, i, :],
+                        lhsT=ident_bf16[:, first + i : first + i + 1].to_broadcast([P, P]),
+                        rhs=b1_sorted[:],
+                        start=True,
+                        stop=True,
+                    )
+                nc.scalar.copy(out=b1_all[:, first : first + 2, :], in_=spread[:])
+            spread = psum_wide.tile([P, ROUND, F2], BF16, tag="wide")
+            nc.tensor.matmul(
+                out=spread[:].rearrange("p a f -> p (a f)"),
+                lhsT=ident_bf16[:, r : r + 1].to_broadcast([P, P]),
+                rhs=b2_rows[:],
+                start=True,
+                stop=True,
+            )
+            nc.scalar.copy(out=b2_all[:, r * ROUND : (r + 1) * ROUND, :], in_=spread[:])
+
+        def place(unit):
+            r = unit // ROUND_UNITS
+            half = (unit // ROUND) % HALVES
+            return r, half, r * ROUND + unit % ROUND
+
+        live = {}
+
+        def transpose_words(bank, source_words):
+            for i in range(UNIT_BLOCKS):
+                for u in range(2):
+                    nc.tensor.transpose(
+                        bank[:, u, i * P : (i + 1) * P], source_words(i, u), ident_f32[:]
+                    )
+
+        def quantise(grouped, name, unit):
+            codes = work.tile([P, UNIT_B], U32, align_bytes=64, tag=name + "_codes")
+            scales = work.tile([P, UNIT_B], U8, align_bytes=64, tag=name + "_scales")
+            nc.vector.quantize_mx(out=codes[:].bitcast(FP8X4), scales=scales[:], in_=grouped[:])
+            live[name + "_codes", unit] = codes
+            live[name + "_scales", unit] = scales
+
+        def transpose_x(unit):
+            r, half, s = place(unit)
+            xt = psum_xt.tile([P, 2, UNIT_B], F32)
+            transpose_words(
+                xt,
+                lambda i, u: x_all[:, r, half * UNIT_BLOCKS + i, s % ROUND, :].bitcast(F32)[
+                    :, u : K // 2 : 2
+                ],
+            )
+            live["xt", unit] = xt
+
+        def group_x(unit):
+            xt = live["xt", unit]
+            x_grouped = work.tile([P, 4 * UNIT_B], BF16, align_bytes=64)
+            nc.scalar.copy(
+                out=x_grouped[:].bitcast(F32).rearrange("p (b u) -> p b u", u=2),
+                in_=xt[:].rearrange("p u b -> p b u"),
+            )
+            live["x_grouped", unit] = x_grouped
+
+        def quantise_x(unit):
+            quantise(live["x_grouped", unit], "x", unit)
+
+        def layer1(unit):
+            r, half, s = place(unit)
+            codes = live["x_codes", unit]
+            scales = live["x_scales", unit]
+            for i in range(UNIT_BLOCKS):
+                cols = slice(i * P, (i + 1) * P)
+                acc = psum_wide.tile([P, F1], F32, tag="wide")
+                nc.tensor.matmul_mx(
+                    out=acc[:],
+                    lhsT=codes[:, cols].bitcast(FP8X4),
+                    lhsT_scale=scales[:, cols],
+                    rhs=w1_all[:, s, :].bitcast(FP8X4),
+                    rhs_scale=w1_planes[:, s, :],
+                    start=True,
+                    stop=True,
+                )
+                live["acc", unit, i] = acc
+
+        def add_bias1(unit):
+            r, half, s = place(unit)
+            h_rows = work.tile([P, UNIT_BLOCKS, F1], BF16)
+            for i in range(UNIT_BLOCKS):
+                acc = live["acc", unit, i]
+                nc.vector.tensor_tensor(
+                    out=h_rows[:, i, :].rearrange("b (u p e) -> b u p e", u=2, e=2),
+                    in0=acc[:].rearrange("b (p u e) -> b u p e", u=2, e=2),
+                    in1=b1_all[:, s, :].rearrange("b (u p e) -> b u p e", u=2, e=2),
+                    op=ADD,
+                )
+            live["h_rows", unit] = h_rows
+
+        def transpose_h(unit):
+            h_rows = live["h_rows", unit]
+            ht = psum_ht.tile([P, 2, UNIT_B], F32)
+            transpose_words(
+                ht, lambda i, u: h_rows[:, i, u * (F1 // 2) : (u + 1) * (F1 // 2)].bitcast(F32)
+            )
+            live["ht", unit] = ht
+
+        def relu_group_h(unit):
+            ht = live["ht", unit]
+            h_grouped = work.tile([P, 4 * UNIT_B], BF16, align_bytes=64)
+            nc.scalar.activation(
+                out=h_grouped[:].rearrange("p (b u e) -> p b u e", u=2, e=2),
+                in_=ht[:]
+                .rearrange("p u b -> p (u b)")
+                .bitcast(BF16)
+                .rearrange("p (u b e) -> p b u e", u=2, e=2),
+                func=RELU,
+            )
+            live["h_grouped", unit] = h_grouped
+
+        def quantise_h(unit):
+            quantise(live["h_grouped", unit], "h", unit)
+
+        def layer2(unit):
+            r, half, s = place(unit)
+            codes = live["h_codes", unit]
+            scales = live["h_scales", unit]
+            y_acc = psum_y.tile([P, UNIT_BLOCKS, F2], F32)
+            for i in range(UNIT_BLOCKS):
+                cols = slice(i * P, (i + 1) * P)
+                nc.tensor.matmul_mx(
+                    out=y_acc[:, i, :],
+                    lhsT=codes[:, cols].bitcast(FP8X4),
+                    lhsT_scale=scales[:, cols],
+                    rhs=w2_all[:, s, :].bitcast(FP8X4),
+                    rhs_scale=w2_planes[:, s, :],
+                    start=True,
+                    stop=True,
+                )
+            live["y_acc", unit] = y_acc
+
+        def add_bias2_and_store(unit):
+            r, half, s = place(unit)
+            a = s % ROUND
+            y_acc = live["y_acc", unit]
+            if a == 0:
+                live["y_rows"] = work.tile([P, UNIT_BLOCKS, ROUND, F2], F32, name="y_rows")
+            y_rows = live["y_rows"]
+            nc.vector.tensor_tensor(
+                out=y_rows[:, :, a, :],
+                in0=y_acc[:],
+                in1=b2_all[:, s, :].unsqueeze(1).to_broadcast([P, UNIT_BLOCKS, F2]),
+                op=ADD,
+            )
+            if a == ROUND - 1:
+                nc.gpsimd.dma_start(
+                    out=out[
+                        half * UNIT_B : (half + 1) * UNIT_B, r * ROUND : (r + 1) * ROUND, :
+                    ].rearrange("(i p) a f -> p i (a f)", p=P),
+                    in_=y_rows[:].rearrange("p i a f -> p i (a f)"),
+                )
+
+        def run(stage, unit):
+            if 0 <= unit < UNITS:
+                stage(unit)
+
+        spread_biases(0)
+        for turn in range(UNITS + LAST_LAG):
+            run(add_bias2_and_store, turn - LAST_LAG)
+            run(quantise_h, turn - 4)
+            run(add_bias1, turn - 2)
+            run(transpose_x, turn)
+            run(transpose_h, turn - 3)
+            run(group_x, turn)
+            run(relu_group_h, turn - 3)
+            run(quantise_x, turn)
+            if turn % ROUND_UNITS == 0 and turn // ROUND_UNITS + 1 < ROUNDS:
+                spread_biases(turn // ROUND_UNITS + 1)
+            run(layer1, turn - 1)
+            run(layer2, turn - 4)

@@ -27,7 +27,7 @@ UNIT_B = UNIT_BLOCKS * P
 HALVES = BLOCKS // UNIT_BLOCKS
 UNITS = STYLES * HALVES
 ROUND_UNITS = ROUND * HALVES
-LAST_LAG = 5
+H_LAG = 3
 QUADRANTS = 4
 
 FLOPS = 2 * STYLES * B * (K * F1 + F1 * F2)
@@ -40,36 +40,31 @@ def tile_simplefusionmodule_pa_t_e_kernel(
     with ExitStack() as stack:
         stack.enter_context(tc.manual_schedule())
         keep = stack.enter_context(tc.tile_pool(name="keep", bufs=1))
-        work = stack.enter_context(tc.tile_pool(name="work", bufs=3))
-        psum_xt = stack.enter_context(tc.psum_pool(name="psum_xt", bufs=2))
-        psum_ht = stack.enter_context(tc.psum_pool(name="psum_ht", bufs=2))
-        psum_wide = stack.enter_context(tc.psum_pool(name="psum_wide", bufs=3))
-        psum_y = stack.enter_context(tc.psum_pool(name="psum_y", bufs=1))
+        work = stack.enter_context(tc.tile_pool(name="work", bufs=4))
+        psum_xt = stack.enter_context(tc.psum_pool(name="psum_xt", bufs=1))
+        psum_ht = stack.enter_context(tc.psum_pool(name="psum_ht", bufs=1))
+        psum_acc = stack.enter_context(tc.psum_pool(name="psum_acc", bufs=4))
+        psum_y = stack.enter_context(tc.psum_pool(name="psum_y", bufs=2))
 
         x_all = keep.tile([P, ROUNDS, BLOCKS, ROUND, K], BF16)
         w1_all = keep.tile([P, STYLES, F1], U32, align_bytes=64)
         w2_all = keep.tile([P, STYLES, F2], U32, align_bytes=64)
         w1_planes = keep.tile([P, STYLES, F1], U8, align_bytes=64)
         w2_planes = keep.tile([P, STYLES, F2], U8, align_bytes=64)
-        b1_rows = keep.tile([P, F1], BF16)
-        b1_sorted = keep.tile([P, F1], BF16)
-        b2_rows = keep.tile([P, ROUND * F2], BF16)
-        b1_all = keep.tile([P, STYLES, F1], BF16)
-        b2_all = keep.tile([P, STYLES, F2], BF16)
+        bias_rows = keep.tile([P, F1 + F2], BF16)
+        bias_sorted = keep.tile([P, F1 + F2], BF16)
+        bias_all = keep.tile([P, STYLES, F1 + F2], BF16)
         ident_f32 = keep.tile([P, P], F32)
         ident_bf16 = keep.tile([P, P], BF16)
 
-        nc.vector.memset(b1_rows[:], 0.0)
-        nc.vector.memset(b2_rows[:], 0.0)
+        nc.vector.memset(bias_rows[:], 0.0)
         nc.vector.memset(w1_planes[:].rearrange("p s n -> p (s n)").bitcast(I32), 0)
         nc.vector.memset(w2_planes[:].rearrange("p s n -> p (s n)").bitcast(I32), 0)
         make_identity(nc, ident_f32[:])
         make_identity(nc, ident_bf16[:])
 
-        nc.scalar.dma_start(out=b1_rows[0:STYLES, :], in_=b1)
-        nc.scalar.dma_start(
-            out=b2_rows[0:ROUNDS, :], in_=b2.rearrange("(r a) f -> r (a f)", a=ROUND)
-        )
+        nc.scalar.dma_start(out=bias_rows[0:STYLES, 0:F1], in_=b1)
+        nc.scalar.dma_start(out=bias_rows[0:STYLES, F1 : F1 + F2], in_=b2)
 
         def load_x(r, block):
             rows = slice(block * P, (block + 1) * P)
@@ -107,39 +102,33 @@ def tile_simplefusionmodule_pa_t_e_kernel(
             load_x(r, 3)
 
         nc.vector.tensor_copy(
-            out=b1_sorted[:].rearrange("s (u p e) -> s u p e", u=2, e=2),
-            in_=b1_rows[:].rearrange("s (p u e) -> s u p e", u=2, e=2),
+            out=bias_sorted[:, 0:F1].rearrange("s (u p e) -> s u p e", u=2, e=2),
+            in_=bias_rows[:, 0:F1].rearrange("s (p u e) -> s u p e", u=2, e=2),
         )
-
-        def spread_biases(r):
-            for pair in range(ROUND // 2):
-                first = r * ROUND + 2 * pair
-                spread = psum_wide.tile([P, 2, F1], BF16, tag="wide")
-                for i in range(2):
-                    nc.tensor.matmul(
-                        out=spread[:, i, :],
-                        lhsT=ident_bf16[:, first + i : first + i + 1].to_broadcast([P, P]),
-                        rhs=b1_sorted[:],
-                        start=True,
-                        stop=True,
-                    )
-                nc.scalar.copy(out=b1_all[:, first : first + 2, :], in_=spread[:])
-            spread = psum_wide.tile([P, ROUND, F2], BF16, tag="wide")
-            nc.tensor.matmul(
-                out=spread[:].rearrange("p a f -> p (a f)"),
-                lhsT=ident_bf16[:, r : r + 1].to_broadcast([P, P]),
-                rhs=b2_rows[:],
-                start=True,
-                stop=True,
-            )
-            nc.scalar.copy(out=b2_all[:, r * ROUND : (r + 1) * ROUND, :], in_=spread[:])
+        nc.vector.tensor_copy(out=bias_sorted[:, F1 : F1 + F2], in_=bias_rows[:, F1 : F1 + F2])
 
         def place(unit):
             r = unit // ROUND_UNITS
             half = (unit // ROUND) % HALVES
             return r, half, r * ROUND + unit % ROUND
 
+        def exists(unit):
+            return 0 <= unit < UNITS
+
         live = {}
+
+        def spread_biases(unit):
+            r, half, s = place(unit)
+            spread = psum_acc.tile([P, F1 + F2], BF16, tag="acc")
+            for cols in (slice(0, F1), slice(F1, F1 + F2)):
+                nc.tensor.matmul(
+                    out=spread[:, cols],
+                    lhsT=ident_bf16[:, s : s + 1].to_broadcast([P, P]),
+                    rhs=bias_sorted[:, cols],
+                    start=True,
+                    stop=True,
+                )
+            nc.scalar.copy(out=bias_all[:, s, :], in_=spread[:])
 
         def transpose_words(bank, source_words):
             for i in range(UNIT_BLOCKS):
@@ -147,13 +136,6 @@ def tile_simplefusionmodule_pa_t_e_kernel(
                     nc.tensor.transpose(
                         bank[:, u, i * P : (i + 1) * P], source_words(i, u), ident_f32[:]
                     )
-
-        def quantise(grouped, name, unit):
-            codes = work.tile([P, UNIT_B], U32, align_bytes=64, tag=name + "_codes")
-            scales = work.tile([P, UNIT_B], U8, align_bytes=64, tag=name + "_scales")
-            nc.vector.quantize_mx(out=codes[:].bitcast(FP8X4), scales=scales[:], in_=grouped[:])
-            live[name + "_codes", unit] = codes
-            live[name + "_scales", unit] = scales
 
         def transpose_x(unit):
             r, half, s = place(unit)
@@ -166,29 +148,51 @@ def tile_simplefusionmodule_pa_t_e_kernel(
             )
             live["xt", unit] = xt
 
-        def group_x(unit):
-            xt = live["xt", unit]
-            x_grouped = work.tile([P, 4 * UNIT_B], BF16, align_bytes=64)
-            nc.scalar.copy(
-                out=x_grouped[:].bitcast(F32).rearrange("p (b u) -> p b u", u=2),
-                in_=xt[:].rearrange("p u b -> p b u"),
+        def transpose_h(unit):
+            h_rows = live["h_rows", unit]
+            ht = psum_ht.tile([P, 2, UNIT_B], F32)
+            transpose_words(
+                ht, lambda i, u: h_rows[:, i, u * (F1 // 2) : (u + 1) * (F1 // 2)].bitcast(F32)
             )
-            live["x_grouped", unit] = x_grouped
+            live["ht", unit] = ht
 
-        def quantise_x(unit):
-            quantise(live["x_grouped", unit], "x", unit)
+        def group_and_quantise(turn):
+            parts = [part for part in range(2) if exists(turn - part * H_LAG)]
+            grouped = work.tile([P, 2, 4 * UNIT_B], BF16, align_bytes=64)
+            codes = work.tile([P, 2, UNIT_B], U32, align_bytes=64)
+            scales = work.tile([P, 2, UNIT_B], U8, align_bytes=64)
+            if 0 in parts:
+                nc.scalar.copy(
+                    out=grouped[:, 0, :].bitcast(F32).rearrange("p (b u) -> p b u", u=2),
+                    in_=live["xt", turn][:].rearrange("p u b -> p b u"),
+                )
+            if 1 in parts:
+                nc.scalar.activation(
+                    out=grouped[:, 1, :].rearrange("p (b u e) -> p b u e", u=2, e=2),
+                    in_=live["ht", turn - H_LAG][:]
+                    .rearrange("p u b -> p (u b)")
+                    .bitcast(BF16)
+                    .rearrange("p (u b e) -> p b u e", u=2, e=2),
+                    func=RELU,
+                )
+            present = slice(parts[0], parts[-1] + 1)
+            nc.vector.quantize_mx(
+                out=codes[:, present, :].rearrange("p c b -> p (c b)").bitcast(FP8X4),
+                scales=scales[:, present, :].rearrange("p c b -> p (c b)"),
+                in_=grouped[:, present, :].rearrange("p c b -> p (c b)"),
+            )
+            live["codes", turn] = codes
+            live["scales", turn] = scales
 
         def layer1(unit):
             r, half, s = place(unit)
-            codes = live["x_codes", unit]
-            scales = live["x_scales", unit]
             for i in range(UNIT_BLOCKS):
                 cols = slice(i * P, (i + 1) * P)
-                acc = psum_wide.tile([P, F1], F32, tag="wide")
+                acc = psum_acc.tile([P, F1], F32, tag="acc")
                 nc.tensor.matmul_mx(
                     out=acc[:],
-                    lhsT=codes[:, cols].bitcast(FP8X4),
-                    lhsT_scale=scales[:, cols],
+                    lhsT=live["codes", unit][:, 0, cols].bitcast(FP8X4),
+                    lhsT_scale=live["scales", unit][:, 0, cols],
                     rhs=w1_all[:, s, :].bitcast(FP8X4),
                     rhs_scale=w1_planes[:, s, :],
                     start=True,
@@ -200,93 +204,63 @@ def tile_simplefusionmodule_pa_t_e_kernel(
             r, half, s = place(unit)
             h_rows = work.tile([P, UNIT_BLOCKS, F1], BF16)
             for i in range(UNIT_BLOCKS):
-                acc = live["acc", unit, i]
                 nc.vector.tensor_tensor(
                     out=h_rows[:, i, :].rearrange("b (u p e) -> b u p e", u=2, e=2),
-                    in0=acc[:].rearrange("b (p u e) -> b u p e", u=2, e=2),
-                    in1=b1_all[:, s, :].rearrange("b (u p e) -> b u p e", u=2, e=2),
+                    in0=live["acc", unit, i][:].rearrange("b (p u e) -> b u p e", u=2, e=2),
+                    in1=bias_all[:, s, 0:F1].rearrange("b (u p e) -> b u p e", u=2, e=2),
                     op=ADD,
                 )
             live["h_rows", unit] = h_rows
 
-        def transpose_h(unit):
-            h_rows = live["h_rows", unit]
-            ht = psum_ht.tile([P, 2, UNIT_B], F32)
-            transpose_words(
-                ht, lambda i, u: h_rows[:, i, u * (F1 // 2) : (u + 1) * (F1 // 2)].bitcast(F32)
-            )
-            live["ht", unit] = ht
-
-        def relu_group_h(unit):
-            ht = live["ht", unit]
-            h_grouped = work.tile([P, 4 * UNIT_B], BF16, align_bytes=64)
-            nc.scalar.activation(
-                out=h_grouped[:].rearrange("p (b u e) -> p b u e", u=2, e=2),
-                in_=ht[:]
-                .rearrange("p u b -> p (u b)")
-                .bitcast(BF16)
-                .rearrange("p (u b e) -> p b u e", u=2, e=2),
-                func=RELU,
-            )
-            live["h_grouped", unit] = h_grouped
-
-        def quantise_h(unit):
-            quantise(live["h_grouped", unit], "h", unit)
-
         def layer2(unit):
             r, half, s = place(unit)
-            codes = live["h_codes", unit]
-            scales = live["h_scales", unit]
-            y_acc = psum_y.tile([P, UNIT_BLOCKS, F2], F32)
+            if unit % 2 == 0:
+                live["y_acc"] = psum_y.tile([P, 2, UNIT_BLOCKS, F2], F32, name="y_acc")
             for i in range(UNIT_BLOCKS):
                 cols = slice(i * P, (i + 1) * P)
                 nc.tensor.matmul_mx(
-                    out=y_acc[:, i, :],
-                    lhsT=codes[:, cols].bitcast(FP8X4),
-                    lhsT_scale=scales[:, cols],
+                    out=live["y_acc"][:, unit % 2, i, :],
+                    lhsT=live["codes", unit + H_LAG][:, 1, cols].bitcast(FP8X4),
+                    lhsT_scale=live["scales", unit + H_LAG][:, 1, cols],
                     rhs=w2_all[:, s, :].bitcast(FP8X4),
                     rhs_scale=w2_planes[:, s, :],
                     start=True,
                     stop=True,
                 )
-            live["y_acc", unit] = y_acc
+            live["y_acc", unit] = live["y_acc"]
 
         def add_bias2_and_store(unit):
             r, half, s = place(unit)
-            a = s % ROUND
-            y_acc = live["y_acc", unit]
-            if a == 0:
-                live["y_rows"] = work.tile([P, UNIT_BLOCKS, ROUND, F2], F32, name="y_rows")
-            y_rows = live["y_rows"]
+            y_rows = work.tile([P, UNIT_BLOCKS, 2, F2], F32)
             nc.vector.tensor_tensor(
-                out=y_rows[:, :, a, :],
-                in0=y_acc[:],
-                in1=b2_all[:, s, :].unsqueeze(1).to_broadcast([P, UNIT_BLOCKS, F2]),
+                out=y_rows[:].rearrange("p i a f -> p a i f"),
+                in0=live["y_acc", unit][:],
+                in1=bias_all[:, s - 1 : s + 1, F1 : F1 + F2]
+                .unsqueeze(2)
+                .to_broadcast([P, 2, UNIT_BLOCKS, F2]),
                 op=ADD,
             )
-            if a == ROUND - 1:
-                nc.gpsimd.dma_start(
-                    out=out[
-                        half * UNIT_B : (half + 1) * UNIT_B, r * ROUND : (r + 1) * ROUND, :
-                    ].rearrange("(i p) a f -> p i (a f)", p=P),
-                    in_=y_rows[:].rearrange("p i a f -> p i (a f)"),
-                )
+            nc.gpsimd.dma_start(
+                out=out[half * UNIT_B : (half + 1) * UNIT_B, s - 1 : s + 1, :].rearrange(
+                    "(i p) a f -> p i (a f)", p=P
+                ),
+                in_=y_rows[:].rearrange("p i a f -> p i (a f)"),
+            )
 
-        def run(stage, unit):
-            if 0 <= unit < UNITS:
-                stage(unit)
-
-        spread_biases(0)
-        for turn in range(UNITS + LAST_LAG):
-            run(add_bias2_and_store, turn - LAST_LAG)
-            run(quantise_h, turn - 4)
-            run(add_bias1, turn - 2)
-            run(transpose_x, turn)
-            run(transpose_h, turn - 3)
-            run(group_x, turn)
-            run(relu_group_h, turn - 3)
-            run(quantise_x, turn)
-            if turn % ROUND_UNITS == 0 and turn // ROUND_UNITS + 1 < ROUNDS:
-                spread_biases(turn // ROUND_UNITS + 1)
-            run(layer1, turn - 1)
-            run(layer2, turn - 4)
+        for turn in range(UNITS + H_LAG + 2):
+            if exists(turn - 2):
+                add_bias1(turn - 2)
+            if exists(turn - H_LAG - 2) and (turn - H_LAG - 2) % 2 == 1:
+                add_bias2_and_store(turn - H_LAG - 2)
+            if exists(turn):
+                transpose_x(turn)
+            if exists(turn - H_LAG):
+                transpose_h(turn - H_LAG)
+            if exists(turn) or exists(turn - H_LAG):
+                group_and_quantise(turn)
+            if exists(turn) and place(turn)[1] == 0:
+                spread_biases(turn)
+            if exists(turn - 1):
+                layer1(turn - 1)
+            if exists(turn - H_LAG - 1):
+                layer2(turn - H_LAG - 1)

@@ -28,6 +28,7 @@ HALVES = BLOCKS // UNIT_BLOCKS
 UNITS = STYLES * HALVES
 ROUND_UNITS = ROUND * HALVES
 H_LAG = 3
+L1_ISSUES = 2
 QUADRANTS = 4
 
 FLOPS = 2 * STYLES * B * (K * F1 + F1 * F2)
@@ -189,15 +190,16 @@ def tile_simplefusionmodule_pa_t_e_kernel(
             for i in range(UNIT_BLOCKS):
                 cols = slice(i * P, (i + 1) * P)
                 acc = psum_acc.tile([P, F1], F32, tag="acc")
-                nc.tensor.matmul_mx(
-                    out=acc[:],
-                    lhsT=live["codes", unit][:, 0, cols].bitcast(FP8X4),
-                    lhsT_scale=live["scales", unit][:, 0, cols],
-                    rhs=w1_all[:, s, :].bitcast(FP8X4),
-                    rhs_scale=w1_planes[:, s, :],
-                    start=True,
-                    stop=True,
-                )
+                for issue in range(L1_ISSUES):
+                    nc.tensor.matmul_mx(
+                        out=acc[:],
+                        lhsT=live["codes", unit][:, 0, cols].bitcast(FP8X4),
+                        lhsT_scale=live["scales", unit][:, 0, cols],
+                        rhs=w1_all[:, s, :].bitcast(FP8X4),
+                        rhs_scale=w1_planes[:, s, :],
+                        start=True,
+                        stop=True,
+                    )
                 live["acc", unit, i] = acc
 
         def add_bias1(unit):

@@ -27,8 +27,7 @@ UNIT_B = UNIT_BLOCKS * P
 HALVES = BLOCKS // UNIT_BLOCKS
 UNITS = STYLES * HALVES
 ROUND_UNITS = ROUND * HALVES
-H_LAG = 3
-L1_ISSUES = 2
+H_LAG = 5
 QUADRANTS = 4
 
 FLOPS = 2 * STYLES * B * (K * F1 + F1 * F2)
@@ -129,7 +128,10 @@ def tile_simplefusionmodule_pa_t_e_kernel(
                     start=True,
                     stop=True,
                 )
-            nc.scalar.copy(out=bias_all[:, s, :], in_=spread[:])
+            live["spread", unit] = spread
+
+        def keep_biases(unit):
+            nc.scalar.copy(out=bias_all[:, place(unit)[2], :], in_=live["spread", unit][:])
 
         def transpose_words(bank, source_words):
             for i in range(UNIT_BLOCKS):
@@ -157,49 +159,51 @@ def tile_simplefusionmodule_pa_t_e_kernel(
             )
             live["ht", unit] = ht
 
-        def group_and_quantise(turn):
-            parts = [part for part in range(2) if exists(turn - part * H_LAG)]
+        def group(number):
             grouped = work.tile([P, 2, 4 * UNIT_B], BF16, align_bytes=64)
-            codes = work.tile([P, 2, UNIT_B], U32, align_bytes=64)
-            scales = work.tile([P, 2, UNIT_B], U8, align_bytes=64)
-            if 0 in parts:
+            if exists(number):
                 nc.scalar.copy(
                     out=grouped[:, 0, :].bitcast(F32).rearrange("p (b u) -> p b u", u=2),
-                    in_=live["xt", turn][:].rearrange("p u b -> p b u"),
+                    in_=live["xt", number][:].rearrange("p u b -> p b u"),
                 )
-            if 1 in parts:
+            if exists(number - H_LAG):
                 nc.scalar.activation(
                     out=grouped[:, 1, :].rearrange("p (b u e) -> p b u e", u=2, e=2),
-                    in_=live["ht", turn - H_LAG][:]
+                    in_=live["ht", number - H_LAG][:]
                     .rearrange("p u b -> p (u b)")
                     .bitcast(BF16)
                     .rearrange("p (u b e) -> p b u e", u=2, e=2),
                     func=RELU,
                 )
+            live["grouped", number] = grouped
+
+        def quantise(number):
+            parts = [part for part in range(2) if exists(number - part * H_LAG)]
             present = slice(parts[0], parts[-1] + 1)
+            codes = work.tile([P, 2, UNIT_B], U32, align_bytes=64)
+            scales = work.tile([P, 2, UNIT_B], U8, align_bytes=64)
             nc.vector.quantize_mx(
                 out=codes[:, present, :].rearrange("p c b -> p (c b)").bitcast(FP8X4),
                 scales=scales[:, present, :].rearrange("p c b -> p (c b)"),
-                in_=grouped[:, present, :].rearrange("p c b -> p (c b)"),
+                in_=live["grouped", number][:, present, :].rearrange("p c b -> p (c b)"),
             )
-            live["codes", turn] = codes
-            live["scales", turn] = scales
+            live["codes", number] = codes
+            live["scales", number] = scales
 
         def layer1(unit):
             r, half, s = place(unit)
             for i in range(UNIT_BLOCKS):
                 cols = slice(i * P, (i + 1) * P)
                 acc = psum_acc.tile([P, F1], F32, tag="acc")
-                for issue in range(L1_ISSUES):
-                    nc.tensor.matmul_mx(
-                        out=acc[:],
-                        lhsT=live["codes", unit][:, 0, cols].bitcast(FP8X4),
-                        lhsT_scale=live["scales", unit][:, 0, cols],
-                        rhs=w1_all[:, s, :].bitcast(FP8X4),
-                        rhs_scale=w1_planes[:, s, :],
-                        start=True,
-                        stop=True,
-                    )
+                nc.tensor.matmul_mx(
+                    out=acc[:],
+                    lhsT=live["codes", unit][:, 0, cols].bitcast(FP8X4),
+                    lhsT_scale=live["scales", unit][:, 0, cols],
+                    rhs=w1_all[:, s, :].bitcast(FP8X4),
+                    rhs_scale=w1_planes[:, s, :],
+                    start=True,
+                    stop=True,
+                )
                 live["acc", unit, i] = acc
 
         def add_bias1(unit):
@@ -249,20 +253,26 @@ def tile_simplefusionmodule_pa_t_e_kernel(
                 in_=y_rows[:].rearrange("p i a f -> p i (a f)"),
             )
 
-        for turn in range(UNITS + H_LAG + 2):
-            if exists(turn - 2):
-                add_bias1(turn - 2)
-            if exists(turn - H_LAG - 2) and (turn - H_LAG - 2) % 2 == 1:
-                add_bias2_and_store(turn - H_LAG - 2)
-            if exists(turn):
-                transpose_x(turn)
-            if exists(turn - H_LAG):
-                transpose_h(turn - H_LAG)
-            if exists(turn) or exists(turn - H_LAG):
-                group_and_quantise(turn)
-            if exists(turn) and place(turn)[1] == 0:
+        def run(stage, unit):
+            if exists(unit):
+                stage(unit)
+
+        def first_of_style(unit):
+            return exists(unit) and place(unit)[1] == 0
+
+        for turn in range(UNITS + H_LAG + 4):
+            run(add_bias1, turn - 4)
+            if (turn - H_LAG - 4) % 2 == 1:
+                run(add_bias2_and_store, turn - H_LAG - 4)
+            if exists(turn - 2) or exists(turn - 2 - H_LAG):
+                quantise(turn - 2)
+            run(transpose_x, turn)
+            run(transpose_h, turn - H_LAG)
+            if first_of_style(turn):
                 spread_biases(turn)
-            if exists(turn - 1):
-                layer1(turn - 1)
-            if exists(turn - H_LAG - 1):
-                layer2(turn - H_LAG - 1)
+            run(layer1, turn - 3)
+            run(layer2, turn - H_LAG - 3)
+            if exists(turn - 1) or exists(turn - 1 - H_LAG):
+                group(turn - 1)
+            if first_of_style(turn - 1):
+                keep_biases(turn - 1)

@@ -19,16 +19,12 @@ D = 256
 K = 2 * D
 F1 = 512
 F2 = 128
-ROUND = 4
-ROUNDS = STYLES // ROUND
+PACK = 4
 BLOCKS = B // P
-UNIT_BLOCKS = 2
-UNIT_B = UNIT_BLOCKS * P
-HALVES = BLOCKS // UNIT_BLOCKS
-UNITS = STYLES * HALVES
-ROUND_UNITS = ROUND * HALVES
-H_LAG = 5
+HALVES = 2
 QUADRANTS = 4
+SHARE = 4
+X_LOADS = (1, 1, 2, 4, 4, 4)
 
 FLOPS = 2 * STYLES * B * (K * F1 + F1 * F2)
 
@@ -40,239 +36,232 @@ def tile_simplefusionmodule_pa_t_e_kernel(
     with ExitStack() as stack:
         stack.enter_context(tc.manual_schedule())
         keep = stack.enter_context(tc.tile_pool(name="keep", bufs=1))
-        work = stack.enter_context(tc.tile_pool(name="work", bufs=4))
-        psum_xt = stack.enter_context(tc.psum_pool(name="psum_xt", bufs=1))
-        psum_ht = stack.enter_context(tc.psum_pool(name="psum_ht", bufs=1))
+        work = stack.enter_context(tc.tile_pool(name="work", bufs=3))
+        psum_xt = stack.enter_context(tc.psum_pool(name="psum_xt", bufs=2))
         psum_acc = stack.enter_context(tc.psum_pool(name="psum_acc", bufs=4))
         psum_y = stack.enter_context(tc.psum_pool(name="psum_y", bufs=2))
 
-        x_all = keep.tile([P, ROUNDS, BLOCKS, ROUND, K], BF16)
+        x_all = keep.tile([P, BLOCKS, STYLES, K], BF16)
+        w1_raw = keep.tile([P, STYLES, F1], U32, align_bytes=64)
         w1_all = keep.tile([P, STYLES, F1], U32, align_bytes=64)
         w2_all = keep.tile([P, STYLES, F2], U32, align_bytes=64)
-        w1_planes = keep.tile([P, STYLES, F1], U8, align_bytes=64)
+        w1_planes_raw = keep.tile([P, STYLES // SHARE, F1], U8, align_bytes=64)
+        w1_planes = keep.tile([P, STYLES // SHARE, F1], U8, align_bytes=64)
         w2_planes = keep.tile([P, STYLES, F2], U8, align_bytes=64)
-        bias_rows = keep.tile([P, F1 + F2], BF16)
-        bias_sorted = keep.tile([P, F1 + F2], BF16)
-        bias_all = keep.tile([P, STYLES, F1 + F2], BF16)
+        b1_bf16 = keep.tile([P, STYLES, PACK], BF16)
+        b1_cols = keep.tile([P, STYLES, PACK], F32)
+        b2_rows = keep.tile([P, F2], BF16)
+        b2_all = keep.tile([P, STYLES, F2], BF16)
         ident_f32 = keep.tile([P, P], F32)
         ident_bf16 = keep.tile([P, P], BF16)
 
-        nc.vector.memset(bias_rows[:], 0.0)
-        nc.vector.memset(w1_planes[:].rearrange("p s n -> p (s n)").bitcast(I32), 0)
+        nc.vector.memset(w1_planes_raw[:].rearrange("p g n -> p (g n)").bitcast(I32), 0)
         nc.vector.memset(w2_planes[:].rearrange("p s n -> p (s n)").bitcast(I32), 0)
+        nc.vector.memset(b2_rows[:], 0.0)
         make_identity(nc, ident_f32[:])
         make_identity(nc, ident_bf16[:])
 
-        nc.scalar.dma_start(out=bias_rows[0:STYLES, 0:F1], in_=b1)
-        nc.scalar.dma_start(out=bias_rows[0:STYLES, F1 : F1 + F2], in_=b2)
+        nc.scalar.dma_start(out=b2_rows[0:STYLES, :], in_=b2)
+        nc.scalar.dma_start(out=b1_bf16[:], in_=b1.rearrange("s (p t) -> p s t", t=PACK))
 
-        def load_x(r, block):
-            rows = slice(block * P, (block + 1) * P)
-            styles = slice(r * ROUND, (r + 1) * ROUND)
-            nc.sync.dma_start(out=x_all[:, r, block, :, 0:D], in_=x1[rows, styles, :])
-            nc.sync.dma_start(out=x_all[:, r, block, :, D:K], in_=x2[rows, styles, :])
+        def load_x(first, count):
+            styles = slice(first, first + count)
+            for block in range(BLOCKS):
+                rows = slice(block * P, (block + 1) * P)
+                nc.sync.dma_start(out=x_all[:, block, styles, 0:D], in_=x1[rows, styles, :])
+                nc.sync.dma_start(out=x_all[:, block, styles, D:K], in_=x2[rows, styles, :])
 
-        def load_scales(planes, scales):
+        def load_w1_scales():
+            for j in range(SHARE):
+                for quadrant in range(QUADRANTS):
+                    first = 32 * quadrant + 4 * j
+                    nc.sync.dma_start(
+                        out=w1_planes_raw[first : first + 4, :, :].bitcast(I32),
+                        in_=W1_scales[j:STYLES:SHARE, 4 * quadrant : 4 * quadrant + 4, :]
+                        .rearrange("g q n -> q g n")
+                        .bitcast(I32),
+                    )
+
+        def load_w2_scales():
             for quadrant in range(QUADRANTS):
                 nc.sync.dma_start(
-                    out=planes[32 * quadrant : 32 * quadrant + 4, :, :].bitcast(I32),
-                    in_=scales[:, 4 * quadrant : 4 * quadrant + 4, :]
+                    out=w2_planes[32 * quadrant : 32 * quadrant + 4, :, :].bitcast(I32),
+                    in_=W2_scales[:, 4 * quadrant : 4 * quadrant + 4, :]
                     .rearrange("s q n -> q s n")
                     .bitcast(I32),
                 )
 
-        def load_words(words_all, words, s):
+        def load_w1(s):
             nc.sync.dma_start(
-                out=words_all[:, s, :].bitcast(I32),
-                in_=words[s].rearrange("p n t -> p (n t)").bitcast(I32),
+                out=w1_raw[:, s, :].bitcast(I32),
+                in_=W1_words[s].rearrange("p n t -> p (n t)").bitcast(I32),
             )
 
-        for r in range(ROUNDS):
-            load_x(r, 0)
-            load_x(r, 1)
-            if r == 0:
-                load_scales(w1_planes, W1_scales)
-            for a in range(ROUND):
-                load_words(w1_all, W1_words, r * ROUND + a)
-            if r == 0:
-                load_scales(w2_planes, W2_scales)
-            for a in range(ROUND):
-                load_words(w2_all, W2_words, r * ROUND + a)
-            load_x(r, 2)
-            load_x(r, 3)
+        def load_w2(first, count):
+            for s in range(first, first + count):
+                nc.sync.dma_start(
+                    out=w2_all[:, s, :].bitcast(I32),
+                    in_=W2_words[s].rearrange("p n t -> p (n t)").bitcast(I32),
+                )
 
-        nc.vector.tensor_copy(
-            out=bias_sorted[:, 0:F1].rearrange("s (u p e) -> s u p e", u=2, e=2),
-            in_=bias_rows[:, 0:F1].rearrange("s (p u e) -> s u p e", u=2, e=2),
-        )
-        nc.vector.tensor_copy(out=bias_sorted[:, F1 : F1 + F2], in_=bias_rows[:, F1 : F1 + F2])
+        first = 0
+        for count in X_LOADS:
+            load_x(first, count)
+            if first == 0:
+                load_w1_scales()
+                load_w2_scales()
+            for s in range(first, first + count):
+                load_w1(s)
+            load_w2(first, count)
+            first += count
 
-        def place(unit):
-            r = unit // ROUND_UNITS
-            half = (unit // ROUND) % HALVES
-            return r, half, r * ROUND + unit % ROUND
-
-        def exists(unit):
-            return 0 <= unit < UNITS
+        nc.vector.tensor_copy(out=b1_cols[:], in_=b1_bf16[:])
+        for half in range(2):
+            spread = psum_acc.tile([P, STYLES // 2, F2], BF16, tag="acc")
+            for a in range(STYLES // 2):
+                s = half * (STYLES // 2) + a
+                nc.tensor.matmul(
+                    out=spread[:, a, :],
+                    lhsT=ident_bf16[:, s : s + 1].to_broadcast([P, P]),
+                    rhs=b2_rows[:],
+                    start=True,
+                    stop=True,
+                )
+            nc.scalar.copy(
+                out=b2_all[:, half * (STYLES // 2) : (half + 1) * (STYLES // 2), :], in_=spread[:]
+            )
 
         live = {}
 
-        def spread_biases(unit):
-            r, half, s = place(unit)
-            spread = psum_acc.tile([P, F1 + F2], BF16, tag="acc")
-            for cols in (slice(0, F1), slice(F1, F1 + F2)):
-                nc.tensor.matmul(
-                    out=spread[:, cols],
-                    lhsT=ident_bf16[:, s : s + 1].to_broadcast([P, P]),
-                    rhs=bias_sorted[:, cols],
-                    start=True,
-                    stop=True,
+        def sort_w1(s):
+            if s % SHARE == 0:
+                g = s // SHARE
+                nc.vector.tensor_copy(
+                    out=w1_planes[:, g, :].rearrange("q (t p) -> q p t", t=PACK),
+                    in_=w1_planes_raw[:, g, :].rearrange("q (p t) -> q p t", t=PACK),
                 )
-            live["spread", unit] = spread
-
-        def keep_biases(unit):
-            nc.scalar.copy(out=bias_all[:, place(unit)[2], :], in_=live["spread", unit][:])
-
-        def transpose_words(bank, source_words):
-            for i in range(UNIT_BLOCKS):
-                for u in range(2):
-                    nc.tensor.transpose(
-                        bank[:, u, i * P : (i + 1) * P], source_words(i, u), ident_f32[:]
-                    )
-
-        def transpose_x(unit):
-            r, half, s = place(unit)
-            xt = psum_xt.tile([P, 2, UNIT_B], F32)
-            transpose_words(
-                xt,
-                lambda i, u: x_all[:, r, half * UNIT_BLOCKS + i, s % ROUND, :].bitcast(F32)[
-                    :, u : K // 2 : 2
-                ],
+            nc.vector.tensor_copy(
+                out=w1_all[:, s, :].bitcast(I32).rearrange("k (t p) -> k t p", t=PACK),
+                in_=w1_raw[:, s, :].bitcast(I32).rearrange("k (p t) -> k t p", t=PACK),
             )
-            live["xt", unit] = xt
 
-        def transpose_h(unit):
-            h_rows = live["h_rows", unit]
-            ht = psum_ht.tile([P, 2, UNIT_B], F32)
-            transpose_words(
-                ht, lambda i, u: h_rows[:, i, u * (F1 // 2) : (u + 1) * (F1 // 2)].bitcast(F32)
-            )
-            live["ht", unit] = ht
+        def transpose_x(s):
+            for half in range(HALVES):
+                xt = psum_xt.tile([P, 2, 2 * P], F32)
+                for i in range(2):
+                    for u in range(2):
+                        nc.tensor.transpose(
+                            xt[:, u, i * P : (i + 1) * P],
+                            x_all[:, 2 * half + i, s, :].bitcast(F32)[:, u : K // 2 : 2],
+                            ident_f32[:],
+                        )
+                live["xt", s, half] = xt
 
-        def group(number):
-            grouped = work.tile([P, 2, 4 * UNIT_B], BF16, align_bytes=64)
-            if exists(number):
+        def group_x(s):
+            grouped = work.tile([P, PACK * B], BF16, align_bytes=64, name="grouped_x")
+            for half in range(HALVES):
                 nc.scalar.copy(
-                    out=grouped[:, 0, :].bitcast(F32).rearrange("p (b u) -> p b u", u=2),
-                    in_=live["xt", number][:].rearrange("p u b -> p b u"),
+                    out=grouped[:, half * 2 * B : (half + 1) * 2 * B]
+                    .bitcast(F32)
+                    .rearrange("p (b u) -> p b u", u=2),
+                    in_=live["xt", s, half][:].rearrange("p u b -> p b u"),
                 )
-            if exists(number - H_LAG):
-                nc.scalar.activation(
-                    out=grouped[:, 1, :].rearrange("p (b u e) -> p b u e", u=2, e=2),
-                    in_=live["ht", number - H_LAG][:]
-                    .rearrange("p u b -> p (u b)")
-                    .bitcast(BF16)
-                    .rearrange("p (u b e) -> p b u e", u=2, e=2),
-                    func=RELU,
-                )
-            live["grouped", number] = grouped
+            live["grouped_x", s] = grouped
 
-        def quantise(number):
-            parts = [part for part in range(2) if exists(number - part * H_LAG)]
-            present = slice(parts[0], parts[-1] + 1)
-            codes = work.tile([P, 2, UNIT_B], U32, align_bytes=64)
-            scales = work.tile([P, 2, UNIT_B], U8, align_bytes=64)
+        def quantise(name, s):
+            codes = work.tile([P, B], U32, align_bytes=64, name="codes_" + name)
+            scales = work.tile([P, B], U8, align_bytes=64, name="scales_" + name)
             nc.vector.quantize_mx(
-                out=codes[:, present, :].rearrange("p c b -> p (c b)").bitcast(FP8X4),
-                scales=scales[:, present, :].rearrange("p c b -> p (c b)"),
-                in_=live["grouped", number][:, present, :].rearrange("p c b -> p (c b)"),
+                out=codes[:].bitcast(FP8X4), scales=scales[:], in_=live["grouped_" + name, s][:]
             )
-            live["codes", number] = codes
-            live["scales", number] = scales
+            live["codes_" + name, s] = codes
+            live["scales_" + name, s] = scales
 
-        def layer1(unit):
-            r, half, s = place(unit)
-            for i in range(UNIT_BLOCKS):
-                cols = slice(i * P, (i + 1) * P)
-                acc = psum_acc.tile([P, F1], F32, tag="acc")
+        def quantise_x(s):
+            quantise("x", s)
+
+        def quantise_h(s):
+            quantise("h", s)
+
+        def layer1(s):
+            g, j = s // SHARE, s % SHARE
+            for t in range(PACK):
+                cols = slice(t * P, (t + 1) * P)
+                acc = psum_acc.tile([P, B], F32, tag="acc")
                 nc.tensor.matmul_mx(
                     out=acc[:],
-                    lhsT=live["codes", unit][:, 0, cols].bitcast(FP8X4),
-                    lhsT_scale=live["scales", unit][:, 0, cols],
-                    rhs=w1_all[:, s, :].bitcast(FP8X4),
-                    rhs_scale=w1_planes[:, s, :],
+                    lhsT=w1_all[:, s, cols].bitcast(FP8X4),
+                    lhsT_scale=w1_planes[4 * j : P, g, cols],
+                    rhs=live["codes_x", s][:].bitcast(FP8X4),
+                    rhs_scale=live["scales_x", s][:],
                     start=True,
                     stop=True,
                 )
-                live["acc", unit, i] = acc
+                live["acc", s, t] = acc
 
-        def add_bias1(unit):
-            r, half, s = place(unit)
-            h_rows = work.tile([P, UNIT_BLOCKS, F1], BF16)
-            for i in range(UNIT_BLOCKS):
-                nc.vector.tensor_tensor(
-                    out=h_rows[:, i, :].rearrange("b (u p e) -> b u p e", u=2, e=2),
-                    in0=live["acc", unit, i][:].rearrange("b (p u e) -> b u p e", u=2, e=2),
-                    in1=bias_all[:, s, 0:F1].rearrange("b (u p e) -> b u p e", u=2, e=2),
-                    op=ADD,
+        def bias1_relu(s):
+            h_rows = work.tile([P, PACK, B], BF16)
+            for t in range(PACK):
+                nc.scalar.activation(
+                    out=h_rows[:, t, :],
+                    in_=live["acc", s, t][:],
+                    func=RELU,
+                    bias=b1_cols[:, s, t : t + 1],
+                    scale=1.0,
                 )
-            live["h_rows", unit] = h_rows
+            live["h_rows", s] = h_rows
 
-        def layer2(unit):
-            r, half, s = place(unit)
-            if unit % 2 == 0:
-                live["y_acc"] = psum_y.tile([P, 2, UNIT_BLOCKS, F2], F32, name="y_acc")
-            for i in range(UNIT_BLOCKS):
+        def group_h(s):
+            grouped = work.tile([P, PACK * B], BF16, align_bytes=64, name="grouped_h")
+            nc.vector.tensor_copy(
+                out=grouped[:].rearrange("p (b t) -> p b t", t=PACK),
+                in_=live["h_rows", s][:].rearrange("p t b -> p b t"),
+            )
+            live["grouped_h", s] = grouped
+
+        def layer2(s):
+            y_acc = psum_y.tile([P, BLOCKS, F2], F32)
+            for i in range(BLOCKS):
                 cols = slice(i * P, (i + 1) * P)
                 nc.tensor.matmul_mx(
-                    out=live["y_acc"][:, unit % 2, i, :],
-                    lhsT=live["codes", unit + H_LAG][:, 1, cols].bitcast(FP8X4),
-                    lhsT_scale=live["scales", unit + H_LAG][:, 1, cols],
+                    out=y_acc[:, i, :],
+                    lhsT=live["codes_h", s][:, cols].bitcast(FP8X4),
+                    lhsT_scale=live["scales_h", s][:, cols],
                     rhs=w2_all[:, s, :].bitcast(FP8X4),
                     rhs_scale=w2_planes[:, s, :],
                     start=True,
                     stop=True,
                 )
-            live["y_acc", unit] = live["y_acc"]
+            live["y_acc", s] = y_acc
 
-        def add_bias2_and_store(unit):
-            r, half, s = place(unit)
-            y_rows = work.tile([P, UNIT_BLOCKS, 2, F2], F32)
+        def bias2_store(s):
+            if s % 2 == 0:
+                live["y_rows"] = work.tile([P, BLOCKS, 2, F2], F32, name="y_rows")
+            y_rows = live["y_rows"]
             nc.vector.tensor_tensor(
-                out=y_rows[:].rearrange("p i a f -> p a i f"),
-                in0=live["y_acc", unit][:],
-                in1=bias_all[:, s - 1 : s + 1, F1 : F1 + F2]
-                .unsqueeze(2)
-                .to_broadcast([P, 2, UNIT_BLOCKS, F2]),
+                out=y_rows[:, :, s % 2, :],
+                in0=live["y_acc", s][:],
+                in1=b2_all[:, s, :].unsqueeze(1).to_broadcast([P, BLOCKS, F2]),
                 op=ADD,
             )
-            nc.gpsimd.dma_start(
-                out=out[half * UNIT_B : (half + 1) * UNIT_B, s - 1 : s + 1, :].rearrange(
-                    "(i p) a f -> p i (a f)", p=P
-                ),
-                in_=y_rows[:].rearrange("p i a f -> p i (a f)"),
-            )
+            if s % 2 == 1:
+                nc.gpsimd.dma_start(
+                    out=out[:, s - 1 : s + 1, :].rearrange("(i p) a f -> p i (a f)", p=P),
+                    in_=y_rows[:].rearrange("p i a f -> p i (a f)"),
+                )
 
-        def run(stage, unit):
-            if exists(unit):
-                stage(unit)
+        def run(stage, s):
+            if 0 <= s < STYLES:
+                stage(s)
 
-        def first_of_style(unit):
-            return exists(unit) and place(unit)[1] == 0
-
-        for turn in range(UNITS + H_LAG + 4):
-            run(add_bias1, turn - 4)
-            if (turn - H_LAG - 4) % 2 == 1:
-                run(add_bias2_and_store, turn - H_LAG - 4)
-            if exists(turn - 2) or exists(turn - 2 - H_LAG):
-                quantise(turn - 2)
-            run(transpose_x, turn)
-            run(transpose_h, turn - H_LAG)
-            if first_of_style(turn):
-                spread_biases(turn)
-            run(layer1, turn - 3)
-            run(layer2, turn - H_LAG - 3)
-            if exists(turn - 1) or exists(turn - 1 - H_LAG):
-                group(turn - 1)
-            if first_of_style(turn - 1):
-                keep_biases(turn - 1)
+        for n in range(-2, STYLES + 2):
+            run(bias2_store, n - 2)
+            run(group_h, n - 1)
+            run(layer1, n)
+            run(bias1_relu, n)
+            run(sort_w1, n + 1)
+            run(quantise_x, n + 1)
+            run(transpose_x, n + 2)
+            run(group_x, n + 2)
+            run(quantise_h, n - 1)
+            run(layer2, n - 1)

@@ -255,13 +255,13 @@ def tile_simplefusionmodule_pa_t_e_kernel(
                 stage(s)
 
         for n in range(-2, STYLES + 2):
-            run(bias2_store, n - 2)
             run(group_h, n - 1)
             run(layer1, n)
             run(bias1_relu, n)
-            run(sort_w1, n + 1)
             run(quantise_x, n + 1)
             run(transpose_x, n + 2)
             run(group_x, n + 2)
             run(quantise_h, n - 1)
             run(layer2, n - 1)
+            run(bias2_store, n - 2)
+            run(sort_w1, n + 2)

@@ -245,7 +245,7 @@ def tile_simplefusionmodule_pa_t_e_kernel(
                 op=ADD,
             )
             if s % 2 == 1:
-                nc.gpsimd.dma_start(
+                nc.sync.dma_start(
                     out=out[:, s - 1 : s + 1, :].rearrange("(i p) a f -> p i (a f)", p=P),
                     in_=y_rows[:].rearrange("p i a f -> p i (a f)"),
                 )

@@ -24,7 +24,7 @@ BLOCKS = B // P
 HALVES = 2
 QUADRANTS = 4
 SHARE = 4
-X_LOADS = (1, 1, 2, 4, 4, 4)
+ROUND = 4
 
 FLOPS = 2 * STYLES * B * (K * F1 + F1 * F2)
 
@@ -41,12 +41,14 @@ def tile_simplefusionmodule_pa_t_e_kernel(
         psum_acc = stack.enter_context(tc.psum_pool(name="psum_acc", bufs=4))
         psum_y = stack.enter_context(tc.psum_pool(name="psum_y", bufs=2))
 
-        x_all = keep.tile([P, BLOCKS, STYLES, K], BF16)
+        x_all = keep.tile([P, STYLES, BLOCKS, K], BF16)
         w1_raw = keep.tile([P, STYLES, F1], U32, align_bytes=64)
         w1_all = keep.tile([P, STYLES, F1], U32, align_bytes=64)
         w2_all = keep.tile([P, STYLES, F2], U32, align_bytes=64)
-        w1_planes_raw = keep.tile([P, STYLES // SHARE, F1], U8, align_bytes=64)
-        w1_planes = keep.tile([P, STYLES // SHARE, F1], U8, align_bytes=64)
+        w1_planes_raw_first = keep.tile([P, SHARE, F1], U8, align_bytes=64)
+        w1_planes_raw_later = keep.tile([P, SHARE, F1], U8, align_bytes=64)
+        w1_planes_first = keep.tile([P, SHARE, F1], U8, align_bytes=64)
+        w1_planes_later = keep.tile([P, SHARE, F1], U8, align_bytes=64)
         w2_planes = keep.tile([P, STYLES, F2], U8, align_bytes=64)
         b1_bf16 = keep.tile([P, STYLES, PACK], BF16)
         b1_cols = keep.tile([P, STYLES, PACK], F32)
@@ -55,7 +57,8 @@ def tile_simplefusionmodule_pa_t_e_kernel(
         ident_f32 = keep.tile([P, P], F32)
         ident_bf16 = keep.tile([P, P], BF16)
 
-        nc.vector.memset(w1_planes_raw[:].rearrange("p g n -> p (g n)").bitcast(I32), 0)
+        nc.vector.memset(w1_planes_raw_first[:].rearrange("p g n -> p (g n)").bitcast(I32), 0)
+        nc.vector.memset(w1_planes_raw_later[:].rearrange("p g n -> p (g n)").bitcast(I32), 0)
         nc.vector.memset(w2_planes[:].rearrange("p s n -> p (s n)").bitcast(I32), 0)
         nc.vector.memset(b2_rows[:], 0.0)
         make_identity(nc, ident_f32[:])
@@ -64,23 +67,24 @@ def tile_simplefusionmodule_pa_t_e_kernel(
         nc.scalar.dma_start(out=b2_rows[0:STYLES, :], in_=b2)
         nc.scalar.dma_start(out=b1_bf16[:], in_=b1.rearrange("s (p t) -> p s t", t=PACK))
 
-        def load_x(first, count):
-            styles = slice(first, first + count)
-            for block in range(BLOCKS):
-                rows = slice(block * P, (block + 1) * P)
-                nc.sync.dma_start(out=x_all[:, block, styles, 0:D], in_=x1[rows, styles, :])
-                nc.sync.dma_start(out=x_all[:, block, styles, D:K], in_=x2[rows, styles, :])
+        def load_x(s):
+            nc.sync.dma_start(
+                out=x_all[:, s, :, 0:D], in_=x1[:, s, :].rearrange("(i p) d -> p i d", p=P)
+            )
+            nc.sync.dma_start(
+                out=x_all[:, s, :, D:K], in_=x2[:, s, :].rearrange("(i p) d -> p i d", p=P)
+            )
 
-        def load_w1_scales():
-            for j in range(SHARE):
-                for quadrant in range(QUADRANTS):
-                    first = 32 * quadrant + 4 * j
-                    nc.sync.dma_start(
-                        out=w1_planes_raw[first : first + 4, :, :].bitcast(I32),
-                        in_=W1_scales[j:STYLES:SHARE, 4 * quadrant : 4 * quadrant + 4, :]
-                        .rearrange("g q n -> q g n")
-                        .bitcast(I32),
-                    )
+        def load_w1_scales(j):
+            raw = w1_planes_raw_first if j == 0 else w1_planes_raw_later
+            for quadrant in range(QUADRANTS):
+                row = 32 * quadrant + 4 * j
+                nc.sync.dma_start(
+                    out=raw[row : row + 4, :, :].bitcast(I32),
+                    in_=W1_scales[SHARE * j : SHARE * (j + 1), 4 * quadrant : 4 * quadrant + 4, :]
+                    .rearrange("g q n -> q g n")
+                    .bitcast(I32),
+                )
 
         def load_w2_scales():
             for quadrant in range(QUADRANTS):
@@ -97,48 +101,36 @@ def tile_simplefusionmodule_pa_t_e_kernel(
                 in_=W1_words[s].rearrange("p n t -> p (n t)").bitcast(I32),
             )
 
-        def load_w2(first, count):
-            for s in range(first, first + count):
-                nc.sync.dma_start(
-                    out=w2_all[:, s, :].bitcast(I32),
-                    in_=W2_words[s].rearrange("p n t -> p (n t)").bitcast(I32),
-                )
-
-        first = 0
-        for count in X_LOADS:
-            load_x(first, count)
-            if first == 0:
-                load_w1_scales()
-                load_w2_scales()
-            for s in range(first, first + count):
-                load_w1(s)
-            load_w2(first, count)
-            first += count
-
-        nc.vector.tensor_copy(out=b1_cols[:], in_=b1_bf16[:])
-        for half in range(2):
-            spread = psum_acc.tile([P, STYLES // 2, F2], BF16, tag="acc")
-            for a in range(STYLES // 2):
-                s = half * (STYLES // 2) + a
-                nc.tensor.matmul(
-                    out=spread[:, a, :],
-                    lhsT=ident_bf16[:, s : s + 1].to_broadcast([P, P]),
-                    rhs=b2_rows[:],
-                    start=True,
-                    stop=True,
-                )
-            nc.scalar.copy(
-                out=b2_all[:, half * (STYLES // 2) : (half + 1) * (STYLES // 2), :], in_=spread[:]
+        def load_w2(s):
+            nc.sync.dma_start(
+                out=w2_all[:, s : s + ROUND, :].bitcast(I32),
+                in_=W2_words[s : s + ROUND].rearrange("s p n t -> p s (n t)").bitcast(I32),
             )
 
+        for s in range(STYLES):
+            load_x(s)
+            if s == 0:
+                load_w1_scales(0)
+            load_w1(s)
+            if s == 1:
+                load_w2_scales()
+            if s % ROUND == 1:
+                load_w2(s - 1)
+            if s == 5:
+                for j in range(1, SHARE):
+                    load_w1_scales(j)
+
+        nc.vector.tensor_copy(out=b1_cols[:], in_=b1_bf16[:])
         live = {}
 
         def sort_w1(s):
-            if s % SHARE == 0:
-                g = s // SHARE
+            if s < 2 * SHARE:
+                g = s % SHARE
+                planes = w1_planes_first if s < SHARE else w1_planes_later
+                raw = w1_planes_raw_first if s < SHARE else w1_planes_raw_later
                 nc.vector.tensor_copy(
-                    out=w1_planes[:, g, :].rearrange("q (t p) -> q p t", t=PACK),
-                    in_=w1_planes_raw[:, g, :].rearrange("q (p t) -> q p t", t=PACK),
+                    out=planes[:, g, :].rearrange("q (t p) -> q p t", t=PACK),
+                    in_=raw[:, g, :].rearrange("q (p t) -> q p t", t=PACK),
                 )
             nc.vector.tensor_copy(
                 out=w1_all[:, s, :].bitcast(I32).rearrange("k (t p) -> k t p", t=PACK),
@@ -152,7 +144,7 @@ def tile_simplefusionmodule_pa_t_e_kernel(
                     for u in range(2):
                         nc.tensor.transpose(
                             xt[:, u, i * P : (i + 1) * P],
-                            x_all[:, 2 * half + i, s, :].bitcast(F32)[:, u : K // 2 : 2],
+                            x_all[:, s, 2 * half + i, :].bitcast(F32)[:, u : K // 2 : 2],
                             ident_f32[:],
                         )
                 live["xt", s, half] = xt
@@ -184,14 +176,15 @@ def tile_simplefusionmodule_pa_t_e_kernel(
             quantise("h", s)
 
         def layer1(s):
-            g, j = s // SHARE, s % SHARE
+            g, j = s % SHARE, s // SHARE
+            planes = w1_planes_first if s < SHARE else w1_planes_later
             for t in range(PACK):
                 cols = slice(t * P, (t + 1) * P)
                 acc = psum_acc.tile([P, B], F32, tag="acc")
                 nc.tensor.matmul_mx(
                     out=acc[:],
                     lhsT=w1_all[:, s, cols].bitcast(FP8X4),
-                    lhsT_scale=w1_planes[4 * j : P, g, cols],
+                    lhsT_scale=planes[4 * j : P, g, cols],
                     rhs=live["codes_x", s][:].bitcast(FP8X4),
                     rhs_scale=live["scales_x", s][:],
                     start=True,
@@ -250,6 +243,27 @@ def tile_simplefusionmodule_pa_t_e_kernel(
                     in_=y_rows[:].rearrange("p i a f -> p i (a f)"),
                 )
 
+        def spread_b2():
+            for half in range(2):
+                spread = psum_y.tile([P, STYLES // 2, F2], BF16, name="y_acc")
+                for a in range(STYLES // 2):
+                    s = half * (STYLES // 2) + a
+                    nc.tensor.matmul(
+                        out=spread[:, a, :],
+                        lhsT=ident_bf16[:, s : s + 1].to_broadcast([P, P]),
+                        rhs=b2_rows[:],
+                        start=True,
+                        stop=True,
+                    )
+                live["spread", half] = spread
+
+        def keep_b2():
+            for half in range(2):
+                nc.vector.tensor_copy(
+                    out=b2_all[:, half * (STYLES // 2) : (half + 1) * (STYLES // 2), :],
+                    in_=live["spread", half][:],
+                )
+
         def run(stage, s):
             if 0 <= s < STYLES:
                 stage(s)
@@ -258,7 +272,11 @@ def tile_simplefusionmodule_pa_t_e_kernel(
             run(group_h, n - 1)
             run(layer1, n)
             run(bias1_relu, n)
+            if n == 0:
+                spread_b2()
             run(quantise_x, n + 1)
+            if n == 0:
+                keep_b2()
             run(transpose_x, n + 2)
             run(group_x, n + 2)
             run(quantise_h, n - 1)

@@ -207,8 +207,8 @@ def tile_simplefusionmodule_pa_t_e_kernel(
         def group_h(s):
             grouped = work.tile([P, PACK * B], BF16, align_bytes=64, name="grouped_h")
             nc.vector.tensor_copy(
-                out=grouped[:].rearrange("p (b t) -> p b t", t=PACK),
-                in_=live["h_rows", s][:].rearrange("p t b -> p b t"),
+                out=grouped[:].rearrange("p (c i t) -> p c t i", i=4, t=PACK),
+                in_=live["h_rows", s][:].rearrange("p t (c i) -> p c t i", i=4),
             )
             live["grouped_h", s] = grouped
 

@@ -25,6 +25,8 @@ HALVES = 2
 QUADRANTS = 4
 SHARE = 4
 ROUND = 4
+LAST_PIECES = 2
+SCALAR_SHARE = 48
 
 FLOPS = 2 * STYLES * B * (K * F1 + F1 * F2)
 
@@ -160,86 +162,109 @@ def tile_simplefusionmodule_pa_t_e_kernel(
                 )
             live["grouped_x", s] = grouped
 
-        def quantise(name, s):
-            codes = work.tile([P, B], U32, align_bytes=64, name="codes_" + name)
-            scales = work.tile([P, B], U8, align_bytes=64, name="scales_" + name)
-            nc.vector.quantize_mx(
-                out=codes[:].bitcast(FP8X4), scales=scales[:], in_=live["grouped_" + name, s][:]
-            )
-            live["codes_" + name, s] = codes
-            live["scales_" + name, s] = scales
+        def pieces(s):
+            return LAST_PIECES if s == STYLES - 1 else 1
 
         def quantise_x(s):
-            quantise("x", s)
+            codes = work.tile([P, B], U32, align_bytes=64, name="codes_x")
+            scales = work.tile([P, B], U8, align_bytes=64, name="scales_x")
+            nc.vector.quantize_mx(
+                out=codes[:].bitcast(FP8X4), scales=scales[:], in_=live["grouped_x", s][:]
+            )
+            live["codes_x", s] = codes
+            live["scales_x", s] = scales
 
-        def quantise_h(s):
-            quantise("h", s)
-
-        def layer1(s):
+        def layer1(s, piece):
             g, j = s % SHARE, s // SHARE
             planes = w1_planes_first if s < SHARE else w1_planes_later
+            width = B // pieces(s)
+            rows = slice(piece * width, (piece + 1) * width)
             for t in range(PACK):
                 cols = slice(t * P, (t + 1) * P)
-                acc = psum_acc.tile([P, B], F32, tag="acc")
+                acc = psum_acc.tile([P, width], F32, tag="acc")
                 nc.tensor.matmul_mx(
                     out=acc[:],
                     lhsT=w1_all[:, s, cols].bitcast(FP8X4),
                     lhsT_scale=planes[4 * j : P, g, cols],
-                    rhs=live["codes_x", s][:].bitcast(FP8X4),
-                    rhs_scale=live["scales_x", s][:],
+                    rhs=live["codes_x", s][:, rows].bitcast(FP8X4),
+                    rhs_scale=live["scales_x", s][:, rows],
                     start=True,
                     stop=True,
                 )
-                live["acc", s, t] = acc
+                live["acc", s, piece, t] = acc
 
-        def bias1_relu(s):
-            h_rows = work.tile([P, PACK, B], BF16)
+        def bias1_relu(s, piece):
+            h_rows = work.tile([P, PACK, B // pieces(s)], BF16)
             for t in range(PACK):
                 nc.scalar.activation(
                     out=h_rows[:, t, :],
-                    in_=live["acc", s, t][:],
+                    in_=live["acc", s, piece, t][:],
                     func=RELU,
                     bias=b1_cols[:, s, t : t + 1],
                     scale=1.0,
                 )
-            live["h_rows", s] = h_rows
+            live["h_rows", s, piece] = h_rows
 
-        def group_h(s):
-            grouped = work.tile([P, PACK * B], BF16, align_bytes=64, name="grouped_h")
+        def layer1_relu(s, piece):
+            layer1(s, piece)
+            bias1_relu(s, piece)
+
+        def group_h(s, piece):
+            grouped = work.tile([P, PACK * B // pieces(s)], BF16, align_bytes=64, name="grouped_h")
+            h_rows = live["h_rows", s, piece]
+            width = B // pieces(s)
+            cut = width - SCALAR_SHARE // pieces(s)
             nc.vector.tensor_copy(
-                out=grouped[:].rearrange("p (c i t) -> p c t i", i=4, t=PACK),
-                in_=live["h_rows", s][:].rearrange("p t (c i) -> p c t i", i=4),
+                out=grouped[:, 0 : PACK * cut].rearrange("p (c i t) -> p c t i", i=4, t=PACK),
+                in_=h_rows[:, :, 0:cut].rearrange("p t (c i) -> p c t i", i=4),
             )
-            live["grouped_h", s] = grouped
+            nc.scalar.copy(
+                out=grouped[:, PACK * cut : PACK * width].rearrange("p (c i t) -> p c t i", i=4, t=PACK),
+                in_=h_rows[:, :, cut:width].rearrange("p t (c i) -> p c t i", i=4),
+            )
+            live["grouped_h", s, piece] = grouped
 
-        def layer2(s):
-            y_acc = psum_y.tile([P, BLOCKS, F2], F32)
-            for i in range(BLOCKS):
+        def quantise_h(s, piece):
+            codes = work.tile([P, B // pieces(s)], U32, align_bytes=64, name="codes_h")
+            scales = work.tile([P, B // pieces(s)], U8, align_bytes=64, name="scales_h")
+            nc.vector.quantize_mx(
+                out=codes[:].bitcast(FP8X4), scales=scales[:], in_=live["grouped_h", s, piece][:]
+            )
+            live["codes_h", s, piece] = codes
+            live["scales_h", s, piece] = scales
+
+        def layer2(s, piece):
+            blocks = BLOCKS // pieces(s)
+            y_acc = psum_y.tile([P, blocks, F2], F32)
+            for i in range(blocks):
                 cols = slice(i * P, (i + 1) * P)
                 nc.tensor.matmul_mx(
                     out=y_acc[:, i, :],
-                    lhsT=live["codes_h", s][:, cols].bitcast(FP8X4),
-                    lhsT_scale=live["scales_h", s][:, cols],
+                    lhsT=live["codes_h", s, piece][:, cols].bitcast(FP8X4),
+                    lhsT_scale=live["scales_h", s, piece][:, cols],
                     rhs=w2_all[:, s, :].bitcast(FP8X4),
                     rhs_scale=w2_planes[:, s, :],
                     start=True,
                     stop=True,
                 )
-            live["y_acc", s] = y_acc
+            live["y_acc", s, piece] = y_acc
 
-        def bias2_store(s):
-            if s % 2 == 0:
-                live["y_rows"] = work.tile([P, BLOCKS, 2, F2], F32, name="y_rows")
+        def bias2_store(s, piece):
+            together = 2 if s < STYLES - 2 else 1
+            blocks = BLOCKS // pieces(s)
+            if s % together == 0:
+                live["y_rows"] = work.tile([P, blocks, together, F2], F32, name="y_rows")
             y_rows = live["y_rows"]
             nc.vector.tensor_tensor(
-                out=y_rows[:, :, s % 2, :],
-                in0=live["y_acc", s][:],
-                in1=b2_all[:, s, :].unsqueeze(1).to_broadcast([P, BLOCKS, F2]),
+                out=y_rows[:, :, s % together, :],
+                in0=live["y_acc", s, piece][:],
+                in1=b2_all[:, s, :].unsqueeze(1).to_broadcast([P, blocks, F2]),
                 op=ADD,
             )
-            if s % 2 == 1:
+            if s % together == together - 1:
+                rows = slice(piece * blocks * P, (piece + 1) * blocks * P)
                 nc.sync.dma_start(
-                    out=out[:, s - 1 : s + 1, :].rearrange("(i p) a f -> p i (a f)", p=P),
+                    out=out[rows, s + 1 - together : s + 1, :].rearrange("(i p) a f -> p i (a f)", p=P),
                     in_=y_rows[:].rearrange("p i a f -> p i (a f)"),
                 )
 
@@ -268,10 +293,14 @@ def tile_simplefusionmodule_pa_t_e_kernel(
             if 0 <= s < STYLES:
                 stage(s)
 
+        def run_pieces(stage, s):
+            if 0 <= s < STYLES:
+                for piece in range(pieces(s)):
+                    stage(s, piece)
+
         for n in range(-2, STYLES + 2):
-            run(group_h, n - 1)
-            run(layer1, n)
-            run(bias1_relu, n)
+            run_pieces(group_h, n - 1)
+            run_pieces(layer1_relu, n)
             if n == 0:
                 spread_b2()
             run(quantise_x, n + 1)
@@ -279,7 +308,7 @@ def tile_simplefusionmodule_pa_t_e_kernel(
                 keep_b2()
             run(transpose_x, n + 2)
             run(group_x, n + 2)
-            run(quantise_h, n - 1)
-            run(layer2, n - 1)
-            run(bias2_store, n - 2)
+            run_pieces(quantise_h, n - 1)
+            run_pieces(layer2, n - 1)
+            run_pieces(bias2_store, n - 2)
             run(sort_w1, n + 2)

@@ -39,6 +39,7 @@ def tile_simplefusionmodule_pa_t_e_kernel(
         stack.enter_context(tc.manual_schedule())
         keep = stack.enter_context(tc.tile_pool(name="keep", bufs=1))
         work = stack.enter_context(tc.tile_pool(name="work", bufs=3))
+        leaving = stack.enter_context(tc.tile_pool(name="leaving", bufs=6))
         psum_xt = stack.enter_context(tc.psum_pool(name="psum_xt", bufs=2))
         psum_acc = stack.enter_context(tc.psum_pool(name="psum_acc", bufs=4))
         psum_y = stack.enter_context(tc.psum_pool(name="psum_y", bufs=2))
@@ -253,7 +254,7 @@ def tile_simplefusionmodule_pa_t_e_kernel(
             together = 2 if s < STYLES - 2 else 1
             blocks = BLOCKS // pieces(s)
             if s % together == 0:
-                live["y_rows"] = work.tile([P, blocks, together, F2], F32, name="y_rows")
+                live["y_rows"] = leaving.tile([P, blocks, together, F2], F32, name="y_rows")
             y_rows = live["y_rows"]
             nc.vector.tensor_tensor(
                 out=y_rows[:, :, s % together, :],

@@ -24,6 +24,7 @@ BLOCKS = B // P
 HALVES = 2
 QUADRANTS = 4
 SHARE = 4
+GROUPS = STYLES // SHARE
 ROUND = 4
 LAST_PIECES = 2
 SCALAR_SHARE = 48
@@ -48,10 +49,8 @@ def tile_simplefusionmodule_pa_t_e_kernel(
         w1_raw = keep.tile([P, STYLES, F1], U32, align_bytes=64)
         w1_all = keep.tile([P, STYLES, F1], U32, align_bytes=64)
         w2_all = keep.tile([P, STYLES, F2], U32, align_bytes=64)
-        w1_planes_raw_first = keep.tile([P, SHARE, F1], U8, align_bytes=64)
-        w1_planes_raw_later = keep.tile([P, SHARE, F1], U8, align_bytes=64)
-        w1_planes_first = keep.tile([P, SHARE, F1], U8, align_bytes=64)
-        w1_planes_later = keep.tile([P, SHARE, F1], U8, align_bytes=64)
+        w1_planes_raw = keep.tile([P, GROUPS, F1], U8, align_bytes=64)
+        w1_planes = keep.tile([P, GROUPS, F1], U8, align_bytes=64)
         w2_planes = keep.tile([P, STYLES, F2], U8, align_bytes=64)
         b1_bf16 = keep.tile([P, STYLES, PACK], BF16)
         b1_cols = keep.tile([P, STYLES, PACK], F32)
@@ -60,8 +59,7 @@ def tile_simplefusionmodule_pa_t_e_kernel(
         ident_f32 = keep.tile([P, P], F32)
         ident_bf16 = keep.tile([P, P], BF16)
 
-        nc.vector.memset(w1_planes_raw_first[:].rearrange("p g n -> p (g n)").bitcast(I32), 0)
-        nc.vector.memset(w1_planes_raw_later[:].rearrange("p g n -> p (g n)").bitcast(I32), 0)
+        nc.vector.memset(w1_planes_raw[:].rearrange("p g n -> p (g n)").bitcast(I32), 0)
         nc.vector.memset(w2_planes[:].rearrange("p s n -> p (s n)").bitcast(I32), 0)
         nc.vector.memset(b2_rows[:], 0.0)
         make_identity(nc, ident_f32[:])
@@ -78,15 +76,12 @@ def tile_simplefusionmodule_pa_t_e_kernel(
                 out=x_all[:, s, :, D:K], in_=x2[:, s, :].rearrange("(i p) d -> p i d", p=P)
             )
 
-        def load_w1_scales(j):
-            raw = w1_planes_raw_first if j == 0 else w1_planes_raw_later
+        def load_w1_scales(g):
             for quadrant in range(QUADRANTS):
-                row = 32 * quadrant + 4 * j
+                row = 32 * quadrant
                 nc.sync.dma_start(
-                    out=raw[row : row + 4, :, :].bitcast(I32),
-                    in_=W1_scales[SHARE * j : SHARE * (j + 1), 4 * quadrant : 4 * quadrant + 4, :]
-                    .rearrange("g q n -> q g n")
-                    .bitcast(I32),
+                    out=w1_planes_raw[row : row + 4 * SHARE, g, :].bitcast(I32),
+                    in_=W1_scales[SHARE * g : SHARE * (g + 1), 4 * quadrant : 4 * quadrant + 4, :].bitcast(I32),
                 )
 
         def load_w2_scales():
@@ -117,27 +112,27 @@ def tile_simplefusionmodule_pa_t_e_kernel(
             load_w1(s)
             if s == 1:
                 load_w2_scales()
+            if s == 2:
+                load_w1_scales(1)
             if s % ROUND == 1:
                 load_w2(s - 1)
             if s == 5:
-                for j in range(1, SHARE):
-                    load_w1_scales(j)
+                for g in range(2, GROUPS):
+                    load_w1_scales(g)
 
         nc.vector.tensor_copy(out=b1_cols[:], in_=b1_bf16[:])
         live = {}
 
         def sort_w1(s):
-            if s < 2 * SHARE:
-                g = s % SHARE
-                planes = w1_planes_first if s < SHARE else w1_planes_later
-                raw = w1_planes_raw_first if s < SHARE else w1_planes_raw_later
+            if s % SHARE == 0:
+                g = s // SHARE
                 nc.vector.tensor_copy(
-                    out=planes[:, g, :].rearrange("q (t p) -> q p t", t=PACK),
-                    in_=raw[:, g, :].rearrange("q (p t) -> q p t", t=PACK),
+                    out=w1_planes[:, g, :].rearrange("q (t p) -> q p t", t=PACK),
+                    in_=w1_planes_raw[:, g, :].rearrange("q (p t) -> q p t", t=PACK),
                 )
             nc.vector.tensor_copy(
-                out=w1_all[:, s, :].bitcast(I32).rearrange("k (t p) -> k t p", t=PACK),
-                in_=w1_raw[:, s, :].bitcast(I32).rearrange("k (p t) -> k t p", t=PACK),
+                out=w1_all[:, s, :].bitcast(I32).rearrange("k (t c i) -> k c t i", t=PACK, i=4),
+                in_=w1_raw[:, s, :].bitcast(I32).rearrange("k (c i t) -> k c t i", i=4, t=PACK),
             )
 
         def transpose_x(s):
@@ -176,8 +171,7 @@ def tile_simplefusionmodule_pa_t_e_kernel(
             live["scales_x", s] = scales
 
         def layer1(s, piece):
-            g, j = s % SHARE, s // SHARE
-            planes = w1_planes_first if s < SHARE else w1_planes_later
+            g, j = s // SHARE, s % SHARE
             width = B // pieces(s)
             rows = slice(piece * width, (piece + 1) * width)
             for t in range(PACK):
@@ -186,7 +180,7 @@ def tile_simplefusionmodule_pa_t_e_kernel(
                 nc.tensor.matmul_mx(
                     out=acc[:],
                     lhsT=w1_all[:, s, cols].bitcast(FP8X4),
-                    lhsT_scale=planes[4 * j : P, g, cols],
+                    lhsT_scale=w1_planes[4 * j : P, g, cols],
                     rhs=live["codes_x", s][:, rows].bitcast(FP8X4),
                     rhs_scale=live["scales_x", s][:, rows],
                     start=True,

@@ -27,7 +27,6 @@ SHARE = 4
 GROUPS = STYLES // SHARE
 ROUND = 4
 LAST_PIECES = 2
-SCALAR_SHARE = 48
 
 FLOPS = 2 * STYLES * B * (K * F1 + F1 * F2)
 
@@ -52,21 +51,24 @@ def tile_simplefusionmodule_pa_t_e_kernel(
         w1_planes_raw = keep.tile([P, GROUPS, F1], U8, align_bytes=64)
         w1_planes = keep.tile([P, GROUPS, F1], U8, align_bytes=64)
         w2_planes = keep.tile([P, STYLES, F2], U8, align_bytes=64)
-        b1_bf16 = keep.tile([P, STYLES, PACK], BF16)
-        b1_cols = keep.tile([P, STYLES, PACK], F32)
-        b2_rows = keep.tile([P, F2], BF16)
+        b1_rows = keep.tile([P, F1], BF16)
+        b1_words = keep.tile([P, STYLES, 2], F32)
+        b1_cols = keep.tile([P, STYLES * PACK], F32)
         b2_all = keep.tile([P, STYLES, F2], BF16)
         ident_f32 = keep.tile([P, P], F32)
-        ident_bf16 = keep.tile([P, P], BF16)
 
+        nc.vector.memset(b1_rows[:].bitcast(I32), 0)
         nc.vector.memset(w1_planes_raw[:].rearrange("p g n -> p (g n)").bitcast(I32), 0)
         nc.vector.memset(w2_planes[:].rearrange("p s n -> p (s n)").bitcast(I32), 0)
-        nc.vector.memset(b2_rows[:], 0.0)
         make_identity(nc, ident_f32[:])
-        make_identity(nc, ident_bf16[:])
 
-        nc.scalar.dma_start(out=b2_rows[0:STYLES, :], in_=b2)
-        nc.scalar.dma_start(out=b1_bf16[:], in_=b1.rearrange("s (p t) -> p s t", t=PACK))
+        nc.scalar.dma_start(out=b1_rows[0:STYLES, :], in_=b1)
+
+        def load_b2():
+            nc.sync.dma_start(
+                out=b2_all[:].rearrange("p s f -> p (s f)"),
+                in_=b2.rearrange("s f -> (s f)").partition_broadcast(P),
+            )
 
         def load_x(s):
             nc.sync.dma_start(
@@ -107,20 +109,21 @@ def tile_simplefusionmodule_pa_t_e_kernel(
 
         for s in range(STYLES):
             load_x(s)
+            load_w1(s)
             if s == 0:
                 load_w1_scales(0)
-            load_w1(s)
             if s == 1:
                 load_w2_scales()
             if s == 2:
                 load_w1_scales(1)
+            if s == 3:
+                load_b2()
             if s % ROUND == 1:
                 load_w2(s - 1)
             if s == 5:
                 for g in range(2, GROUPS):
                     load_w1_scales(g)
 
-        nc.vector.tensor_copy(out=b1_cols[:], in_=b1_bf16[:])
         live = {}
 
         def sort_w1(s):
@@ -195,7 +198,7 @@ def tile_simplefusionmodule_pa_t_e_kernel(
                     out=h_rows[:, t, :],
                     in_=live["acc", s, piece, t][:],
                     func=RELU,
-                    bias=b1_cols[:, s, t : t + 1],
+                    bias=b1_cols[:, PACK * s + t : PACK * s + t + 1],
                     scale=1.0,
                 )
             live["h_rows", s, piece] = h_rows
@@ -207,15 +210,9 @@ def tile_simplefusionmodule_pa_t_e_kernel(
         def group_h(s, piece):
             grouped = work.tile([P, PACK * B // pieces(s)], BF16, align_bytes=64, name="grouped_h")
             h_rows = live["h_rows", s, piece]
-            width = B // pieces(s)
-            cut = width - SCALAR_SHARE // pieces(s)
             nc.vector.tensor_copy(
-                out=grouped[:, 0 : PACK * cut].rearrange("p (c i t) -> p c t i", i=4, t=PACK),
-                in_=h_rows[:, :, 0:cut].rearrange("p t (c i) -> p c t i", i=4),
-            )
-            nc.scalar.copy(
-                out=grouped[:, PACK * cut : PACK * width].rearrange("p (c i t) -> p c t i", i=4, t=PACK),
-                in_=h_rows[:, :, cut:width].rearrange("p t (c i) -> p c t i", i=4),
+                out=grouped[:].rearrange("p (c i t) -> p c t i", i=4, t=PACK),
+                in_=h_rows[:].rearrange("p t (c i) -> p c t i", i=4),
             )
             live["grouped_h", s, piece] = grouped
 
@@ -263,26 +260,19 @@ def tile_simplefusionmodule_pa_t_e_kernel(
                     in_=y_rows[:].rearrange("p i a f -> p i (a f)"),
                 )
 
-        def spread_b2():
-            for half in range(2):
-                spread = psum_y.tile([P, STYLES // 2, F2], BF16, name="y_acc")
-                for a in range(STYLES // 2):
-                    s = half * (STYLES // 2) + a
-                    nc.tensor.matmul(
-                        out=spread[:, a, :],
-                        lhsT=ident_bf16[:, s : s + 1].to_broadcast([P, P]),
-                        rhs=b2_rows[:],
-                        start=True,
-                        stop=True,
-                    )
-                live["spread", half] = spread
+        def transpose_b1():
+            turned = psum_y.tile([P, 2, P], F32, name="y_acc")
+            for u in range(2):
+                nc.tensor.transpose(turned[:, u, :], b1_rows[:].bitcast(F32)[:, u : F1 // 2 : 2], ident_f32[:])
+            live["turned_b1"] = turned
 
-        def keep_b2():
-            for half in range(2):
-                nc.vector.tensor_copy(
-                    out=b2_all[:, half * (STYLES // 2) : (half + 1) * (STYLES // 2), :],
-                    in_=live["spread", half][:],
-                )
+        def keep_b1():
+            nc.vector.tensor_copy(
+                out=b1_words[:], in_=live["turned_b1"][:, :, 0:STYLES].rearrange("p u s -> p s u")
+            )
+            nc.vector.tensor_copy(
+                out=b1_cols[:], in_=b1_words[:].rearrange("p s u -> p (s u)").bitcast(BF16)
+            )
 
         def run(stage, s):
             if 0 <= s < STYLES:
@@ -296,11 +286,10 @@ def tile_simplefusionmodule_pa_t_e_kernel(
         for n in range(-2, STYLES + 2):
             run_pieces(group_h, n - 1)
             run_pieces(layer1_relu, n)
-            if n == 0:
-                spread_b2()
             run(quantise_x, n + 1)
-            if n == 0:
-                keep_b2()
+            if n == -1:
+                transpose_b1()
+                keep_b1()
             run(transpose_x, n + 2)
             run(group_x, n + 2)
             run_pieces(quantise_h, n - 1)

@@ -70,13 +70,16 @@ def tile_simplefusionmodule_pa_t_e_kernel(
                 in_=b2.rearrange("s f -> (s f)").partition_broadcast(P),
             )
 
-        def load_x(s):
-            nc.sync.dma_start(
-                out=x_all[:, s, :, 0:D], in_=x1[:, s, :].rearrange("(i p) d -> p i d", p=P)
-            )
-            nc.sync.dma_start(
-                out=x_all[:, s, :, D:K], in_=x2[:, s, :].rearrange("(i p) d -> p i d", p=P)
-            )
+        def load_x(s, parts=1):
+            blocks = BLOCKS // parts
+            for part in range(parts):
+                first = part * blocks
+                rows = slice(first * P, (first + blocks) * P)
+                for stream, source in enumerate((x1, x2)):
+                    nc.sync.dma_start(
+                        out=x_all[:, s, first : first + blocks, stream * D : (stream + 1) * D],
+                        in_=source[rows, s, :].rearrange("(i p) d -> p i d", p=P),
+                    )
 
         def load_w1_scales(g):
             for quadrant in range(QUADRANTS):
@@ -107,32 +110,35 @@ def tile_simplefusionmodule_pa_t_e_kernel(
                 in_=W2_words[s : s + ROUND].rearrange("s p n t -> p s (n t)").bitcast(I32),
             )
 
-        for s in range(STYLES):
+        load_x(0, parts=2)
+        load_w1(0)
+        load_x(1)
+        load_w1_scales(0)
+        load_w1(1)
+        for s in range(2, STYLES):
             load_x(s)
             load_w1(s)
-            if s == 0:
-                load_w1_scales(0)
-            if s == 1:
-                load_w2_scales()
             if s == 2:
-                load_w1_scales(1)
+                load_w2_scales()
             if s == 3:
+                load_w1_scales(1)
+            if s == 4:
                 load_b2()
-            if s % ROUND == 1:
-                load_w2(s - 1)
-            if s == 5:
-                for g in range(2, GROUPS):
-                    load_w1_scales(g)
+            if s == 7:
+                load_w1_scales(2)
+                load_w1_scales(3)
+            if s % ROUND == 2:
+                load_w2(s - 2)
 
         live = {}
 
+        def sort_w1_scales(g):
+            nc.vector.tensor_copy(
+                out=w1_planes[:, g, :].rearrange("q (t p) -> q p t", t=PACK),
+                in_=w1_planes_raw[:, g, :].rearrange("q (p t) -> q p t", t=PACK),
+            )
+
         def sort_w1(s):
-            if s % SHARE == 0:
-                g = s // SHARE
-                nc.vector.tensor_copy(
-                    out=w1_planes[:, g, :].rearrange("q (t p) -> q p t", t=PACK),
-                    in_=w1_planes_raw[:, g, :].rearrange("q (p t) -> q p t", t=PACK),
-                )
             nc.vector.tensor_copy(
                 out=w1_all[:, s, :].bitcast(I32).rearrange("k (t c i) -> k c t i", t=PACK, i=4),
                 in_=w1_raw[:, s, :].bitcast(I32).rearrange("k (c i t) -> k c t i", i=4, t=PACK),
@@ -288,6 +294,7 @@ def tile_simplefusionmodule_pa_t_e_kernel(
             run_pieces(layer1_relu, n)
             run(quantise_x, n + 1)
             if n == -1:
+                sort_w1_scales(0)
                 transpose_b1()
                 keep_b1()
             run(transpose_x, n + 2)
@@ -295,4 +302,6 @@ def tile_simplefusionmodule_pa_t_e_kernel(
             run_pieces(quantise_h, n - 1)
             run_pieces(layer2, n - 1)
             run_pieces(bias2_store, n - 2)
+            if 0 < n + 2 < STYLES and (n + 2) % SHARE == 0:
+                sort_w1_scales((n + 2) // SHARE)
             run(sort_w1, n + 2)

@@ -54,21 +54,20 @@ def tile_simplefusionmodule_pa_t_e_kernel(
         b1_rows = keep.tile([P, F1], BF16)
         b1_words = keep.tile([P, STYLES, 2], F32)
         b1_cols = keep.tile([P, STYLES * PACK], F32)
+        b2_rows = keep.tile([P, F2], BF16)
         b2_all = keep.tile([P, STYLES, F2], BF16)
         ident_f32 = keep.tile([P, P], F32)
+        ident_bf16 = keep.tile([P, P], BF16)
 
         nc.vector.memset(b1_rows[:].bitcast(I32), 0)
+        nc.vector.memset(b2_rows[:].bitcast(I32), 0)
         nc.vector.memset(w1_planes_raw[:].rearrange("p g n -> p (g n)").bitcast(I32), 0)
         nc.vector.memset(w2_planes[:].rearrange("p s n -> p (s n)").bitcast(I32), 0)
         make_identity(nc, ident_f32[:])
+        make_identity(nc, ident_bf16[:])
 
         nc.scalar.dma_start(out=b1_rows[0:STYLES, :], in_=b1)
-
-        def load_b2():
-            nc.sync.dma_start(
-                out=b2_all[:].rearrange("p s f -> p (s f)"),
-                in_=b2.rearrange("s f -> (s f)").partition_broadcast(P),
-            )
+        nc.scalar.dma_start(out=b2_rows[0:STYLES, :], in_=b2)
 
         def load_x(s, parts=1):
             blocks = BLOCKS // parts
@@ -122,8 +121,6 @@ def tile_simplefusionmodule_pa_t_e_kernel(
                 load_w2_scales()
             if s == 3:
                 load_w1_scales(1)
-            if s == 4:
-                load_b2()
             if s == 7:
                 load_w1_scales(2)
                 load_w1_scales(3)
@@ -267,7 +264,7 @@ def tile_simplefusionmodule_pa_t_e_kernel(
                 )
 
         def transpose_b1():
-            turned = psum_y.tile([P, 2, P], F32, name="y_acc")
+            turned = psum_acc.tile([P, 2, P], F32, tag="acc")
             for u in range(2):
                 nc.tensor.transpose(turned[:, u, :], b1_rows[:].bitcast(F32)[:, u : F1 // 2 : 2], ident_f32[:])
             live["turned_b1"] = turned
@@ -279,6 +276,22 @@ def tile_simplefusionmodule_pa_t_e_kernel(
             nc.vector.tensor_copy(
                 out=b1_cols[:], in_=b1_words[:].rearrange("p s u -> p (s u)").bitcast(BF16)
             )
+
+        def spread_b2():
+            for half in range(2):
+                spread = psum_y.tile([P, STYLES // 2, F2], BF16, name="y_acc")
+                for a in range(STYLES // 2):
+                    s = half * (STYLES // 2) + a
+                    nc.tensor.matmul(
+                        out=spread[:, a, :],
+                        lhsT=ident_bf16[:, s : s + 1].to_broadcast([P, P]),
+                        rhs=b2_rows[:],
+                        start=True,
+                        stop=True,
+                    )
+                nc.vector.tensor_copy(
+                    out=b2_all[:, half * (STYLES // 2) : (half + 1) * (STYLES // 2), :], in_=spread[:]
+                )
 
         def run(stage, s):
             if 0 <= s < STYLES:
@@ -297,6 +310,8 @@ def tile_simplefusionmodule_pa_t_e_kernel(
                 sort_w1_scales(0)
                 transpose_b1()
                 keep_b1()
+            if n == 0:
+                spread_b2()
             run(transpose_x, n + 2)
             run(group_x, n + 2)
             run_pieces(quantise_h, n - 1)

@@ -213,10 +213,17 @@ def tile_simplefusionmodule_pa_t_e_kernel(
         def group_h(s, piece):
             grouped = work.tile([P, PACK * B // pieces(s)], BF16, align_bytes=64, name="grouped_h")
             h_rows = live["h_rows", s, piece]
+            width = B // pieces(s)
+            cut = width // 2 if s == STYLES - 1 else width
             nc.vector.tensor_copy(
-                out=grouped[:].rearrange("p (c i t) -> p c t i", i=4, t=PACK),
-                in_=h_rows[:].rearrange("p t (c i) -> p c t i", i=4),
+                out=grouped[:, 0 : PACK * cut].rearrange("p (c i v w) -> p c v i w", i=4, v=2, w=2),
+                in_=h_rows[:, :, 0:cut].rearrange("p (v w) (c i) -> p c v i w", v=2, i=4),
             )
+            if cut < width:
+                nc.scalar.copy(
+                    out=grouped[:, PACK * cut : PACK * width].rearrange("p (c i t) -> p c t i", i=4, t=PACK),
+                    in_=h_rows[:, :, cut:width].rearrange("p t (c i) -> p c t i", i=4),
+                )
             live["grouped_h", s, piece] = grouped
 
         def quantise_h(s, piece):
@@ -302,9 +309,10 @@ def tile_simplefusionmodule_pa_t_e_kernel(
                 for piece in range(pieces(s)):
                     stage(s, piece)
 
-        for n in range(-2, STYLES + 2):
+        for n in range(-2, STYLES):
             run_pieces(group_h, n - 1)
             run_pieces(layer1_relu, n)
+            run_pieces(layer2, n - 2)
             run(quantise_x, n + 1)
             if n == -1:
                 sort_w1_scales(0)
@@ -315,8 +323,19 @@ def tile_simplefusionmodule_pa_t_e_kernel(
             run(transpose_x, n + 2)
             run(group_x, n + 2)
             run_pieces(quantise_h, n - 1)
-            run_pieces(layer2, n - 1)
             run_pieces(bias2_store, n - 2)
             if 0 < n + 2 < STYLES and (n + 2) % SHARE == 0:
                 sort_w1_scales((n + 2) // SHARE)
             run(sort_w1, n + 2)
+
+        last = STYLES - 1
+        layer2(last - 1, 0)
+        group_h(last, 0)
+        bias2_store(last - 1, 0)
+        for piece in range(LAST_PIECES):
+            if piece > 0:
+                group_h(last, piece)
+            quantise_h(last, piece)
+            layer2(last, piece)
+        for piece in range(LAST_PIECES):
+            bias2_store(last, piece)

@@ -137,8 +137,8 @@ def tile_simplefusionmodule_pa_t_e_kernel(
 
         def sort_w1(s):
             nc.vector.tensor_copy(
-                out=w1_all[:, s, :].bitcast(I32).rearrange("k (t c i) -> k c t i", t=PACK, i=4),
-                in_=w1_raw[:, s, :].bitcast(I32).rearrange("k (c i t) -> k c t i", i=4, t=PACK),
+                out=w1_all[:, s, :].bitcast(I32).rearrange("k (v w c i) -> k c v i w", v=2, w=2, i=4),
+                in_=w1_raw[:, s, :].bitcast(I32).rearrange("k (c i v w) -> k c v i w", i=4, v=2, w=2),
             )
 
         def transpose_x(s):

from contextlib import ExitStack

import concourse.mybir as mybir
from concourse.masks import make_identity

F32 = mybir.dt.float32
BF16 = mybir.dt.bfloat16
I32 = mybir.dt.int32
U32 = mybir.dt.uint32
U8 = mybir.dt.uint8
FP8X4 = mybir.dt.float8_e4m3fn_x4
ADD = mybir.AluOpType.add
RELU = mybir.ActivationFunctionType.Relu

P = 128
B = 512
STYLES = 16
D = 256
K = 2 * D
F1 = 512
F2 = 128
PACK = 4
BLOCKS = B // P
HALVES = 2
QUADRANTS = 4
SHARE = 4
GROUPS = STYLES // SHARE
ROUND = 4
LAST_PIECES = 2

FLOPS = 2 * STYLES * B * (K * F1 + F1 * F2)


def tile_simplefusionmodule_pa_t_e_kernel(
    tc, x1, x2, W1_words, W1_scales, b1, W2_words, W2_scales, b2, out
):
    nc = tc.nc
    with ExitStack() as stack:
        stack.enter_context(tc.manual_schedule())
        keep = stack.enter_context(tc.tile_pool(name="keep", bufs=1))
        work = stack.enter_context(tc.tile_pool(name="work", bufs=3))
        leaving = stack.enter_context(tc.tile_pool(name="leaving", bufs=6))
        psum_xt = stack.enter_context(tc.psum_pool(name="psum_xt", bufs=2))
        psum_acc = stack.enter_context(tc.psum_pool(name="psum_acc", bufs=4))
        psum_y = stack.enter_context(tc.psum_pool(name="psum_y", bufs=2))

        x_all = keep.tile([P, STYLES, BLOCKS, K], BF16)
        w1_raw = keep.tile([P, STYLES, F1], U32, align_bytes=64)
        w1_all = keep.tile([P, STYLES, F1], U32, align_bytes=64)
        w2_all = keep.tile([P, STYLES, F2], U32, align_bytes=64)
        w1_planes_raw = keep.tile([P, GROUPS, F1], U8, align_bytes=64)
        w1_planes = keep.tile([P, GROUPS, F1], U8, align_bytes=64)
        w2_planes = keep.tile([P, STYLES, F2], U8, align_bytes=64)
        b1_rows = keep.tile([P, F1], BF16)
        b1_words = keep.tile([P, STYLES, 2], F32)
        b1_cols = keep.tile([P, STYLES * PACK], F32)
        b2_rows = keep.tile([P, F2], BF16)
        b2_all = keep.tile([P, STYLES, F2], BF16)
        ident_f32 = keep.tile([P, P], F32)
        ident_bf16 = keep.tile([P, P], BF16)

        nc.vector.memset(b1_rows[:].bitcast(I32), 0)
        nc.vector.memset(b2_rows[:].bitcast(I32), 0)
        nc.vector.memset(w1_planes_raw[:].rearrange("p g n -> p (g n)").bitcast(I32), 0)
        nc.vector.memset(w2_planes[:].rearrange("p s n -> p (s n)").bitcast(I32), 0)
        make_identity(nc, ident_f32[:])
        make_identity(nc, ident_bf16[:])

        nc.scalar.dma_start(out=b1_rows[0:STYLES, :], in_=b1)
        nc.scalar.dma_start(out=b2_rows[0:STYLES, :], in_=b2)

        def load_x(s, parts=1):
            blocks = BLOCKS // parts
            for part in range(parts):
                first = part * blocks
                rows = slice(first * P, (first + blocks) * P)
                for stream, source in enumerate((x1, x2)):
                    nc.sync.dma_start(
                        out=x_all[:, s, first : first + blocks, stream * D : (stream + 1) * D],
                        in_=source[rows, s, :].rearrange("(i p) d -> p i d", p=P),
                    )

        def load_w1_scales(g):
            for quadrant in range(QUADRANTS):
                row = 32 * quadrant
                nc.sync.dma_start(
                    out=w1_planes_raw[row : row + 4 * SHARE, g, :].bitcast(I32),
                    in_=W1_scales[SHARE * g : SHARE * (g + 1), 4 * quadrant : 4 * quadrant + 4, :].bitcast(I32),
                )

        def load_w2_scales():
            for quadrant in range(QUADRANTS):
                nc.sync.dma_start(
                    out=w2_planes[32 * quadrant : 32 * quadrant + 4, :, :].bitcast(I32),
                    in_=W2_scales[:, 4 * quadrant : 4 * quadrant + 4, :]
                    .rearrange("s q n -> q s n")
                    .bitcast(I32),
                )

        def load_w1(s):
            nc.sync.dma_start(
                out=w1_raw[:, s, :].bitcast(I32),
                in_=W1_words[s].rearrange("p n t -> p (n t)").bitcast(I32),
            )

        def load_w2(s):
            nc.sync.dma_start(
                out=w2_all[:, s : s + ROUND, :].bitcast(I32),
                in_=W2_words[s : s + ROUND].rearrange("s p n t -> p s (n t)").bitcast(I32),
            )

        load_x(0, parts=2)
        load_w1(0)
        load_x(1)
        load_w1_scales(0)
        load_w1(1)
        for s in range(2, STYLES):
            load_x(s)
            load_w1(s)
            if s == 2:
                load_w2_scales()
            if s == 3:
                load_w1_scales(1)
            if s == 7:
                load_w1_scales(2)
                load_w1_scales(3)
            if s % ROUND == 2:
                load_w2(s - 2)

        live = {}

        def sort_w1_scales(g):
            nc.vector.tensor_copy(
                out=w1_planes[:, g, :].rearrange("q (t p) -> q p t", t=PACK),
                in_=w1_planes_raw[:, g, :].rearrange("q (p t) -> q p t", t=PACK),
            )

        def sort_w1(s):
            nc.vector.tensor_copy(
                out=w1_all[:, s, :].bitcast(I32).rearrange("k (v w c i) -> k c v i w", v=2, w=2, i=4),
                in_=w1_raw[:, s, :].bitcast(I32).rearrange("k (c i v w) -> k c v i w", i=4, v=2, w=2),
            )

        def transpose_x(s):
            for half in range(HALVES):
                xt = psum_xt.tile([P, 2, 2 * P], F32)
                for i in range(2):
                    for u in range(2):
                        nc.tensor.transpose(
                            xt[:, u, i * P : (i + 1) * P],
                            x_all[:, s, 2 * half + i, :].bitcast(F32)[:, u : K // 2 : 2],
                            ident_f32[:],
                        )
                live["xt", s, half] = xt

        def group_x(s):
            grouped = work.tile([P, PACK * B], BF16, align_bytes=64, name="grouped_x")
            for half in range(HALVES):
                nc.scalar.copy(
                    out=grouped[:, half * 2 * B : (half + 1) * 2 * B]
                    .bitcast(F32)
                    .rearrange("p (b u) -> p b u", u=2),
                    in_=live["xt", s, half][:].rearrange("p u b -> p b u"),
                )
            live["grouped_x", s] = grouped

        def pieces(s):
            return LAST_PIECES if s == STYLES - 1 else 1

        def quantise_x(s):
            codes = work.tile([P, B], U32, align_bytes=64, name="codes_x")
            scales = work.tile([P, B], U8, align_bytes=64, name="scales_x")
            nc.vector.quantize_mx(
                out=codes[:].bitcast(FP8X4), scales=scales[:], in_=live["grouped_x", s][:]
            )
            live["codes_x", s] = codes
            live["scales_x", s] = scales

        def layer1(s, piece):
            g, j = s // SHARE, s % SHARE
            width = B // pieces(s)
            rows = slice(piece * width, (piece + 1) * width)
            for t in range(PACK):
                cols = slice(t * P, (t + 1) * P)
                acc = psum_acc.tile([P, width], F32, tag="acc")
                nc.tensor.matmul_mx(
                    out=acc[:],
                    lhsT=w1_all[:, s, cols].bitcast(FP8X4),
                    lhsT_scale=w1_planes[4 * j : P, g, cols],
                    rhs=live["codes_x", s][:, rows].bitcast(FP8X4),
                    rhs_scale=live["scales_x", s][:, rows],
                    start=True,
                    stop=True,
                )
                live["acc", s, piece, t] = acc

        def bias1_relu(s, piece):
            h_rows = work.tile([P, PACK, B // pieces(s)], BF16)
            for t in range(PACK):
                nc.scalar.activation(
                    out=h_rows[:, t, :],
                    in_=live["acc", s, piece, t][:],
                    func=RELU,
                    bias=b1_cols[:, PACK * s + t : PACK * s + t + 1],
                    scale=1.0,
                )
            live["h_rows", s, piece] = h_rows

        def layer1_relu(s, piece):
            layer1(s, piece)
            bias1_relu(s, piece)

        def group_h(s, piece):
            grouped = work.tile([P, PACK * B // pieces(s)], BF16, align_bytes=64, name="grouped_h")
            h_rows = live["h_rows", s, piece]
            width = B // pieces(s)
            cut = width // 2 if s == STYLES - 1 else width
            nc.vector.tensor_copy(
                out=grouped[:, 0 : PACK * cut].rearrange("p (c i v w) -> p c v i w", i=4, v=2, w=2),
                in_=h_rows[:, :, 0:cut].rearrange("p (v w) (c i) -> p c v i w", v=2, i=4),
            )
            if cut < width:
                nc.scalar.copy(
                    out=grouped[:, PACK * cut : PACK * width].rearrange("p (c i t) -> p c t i", i=4, t=PACK),
                    in_=h_rows[:, :, cut:width].rearrange("p t (c i) -> p c t i", i=4),
                )
            live["grouped_h", s, piece] = grouped

        def quantise_h(s, piece):
            codes = work.tile([P, B // pieces(s)], U32, align_bytes=64, name="codes_h")
            scales = work.tile([P, B // pieces(s)], U8, align_bytes=64, name="scales_h")
            nc.vector.quantize_mx(
                out=codes[:].bitcast(FP8X4), scales=scales[:], in_=live["grouped_h", s, piece][:]
            )
            live["codes_h", s, piece] = codes
            live["scales_h", s, piece] = scales

        def layer2(s, piece):
            blocks = BLOCKS // pieces(s)
            y_acc = psum_y.tile([P, blocks, F2], F32)
            for i in range(blocks):
                cols = slice(i * P, (i + 1) * P)
                nc.tensor.matmul_mx(
                    out=y_acc[:, i, :],
                    lhsT=live["codes_h", s, piece][:, cols].bitcast(FP8X4),
                    lhsT_scale=live["scales_h", s, piece][:, cols],
                    rhs=w2_all[:, s, :].bitcast(FP8X4),
                    rhs_scale=w2_planes[:, s, :],
                    start=True,
                    stop=True,
                )
            live["y_acc", s, piece] = y_acc

        def bias2_store(s, piece):
            together = 2 if s < STYLES - 2 else 1
            blocks = BLOCKS // pieces(s)
            if s % together == 0:
                live["y_rows"] = leaving.tile([P, blocks, together, F2], F32, name="y_rows")
            y_rows = live["y_rows"]
            nc.vector.tensor_tensor(
                out=y_rows[:, :, s % together, :],
                in0=live["y_acc", s, piece][:],
                in1=b2_all[:, s, :].unsqueeze(1).to_broadcast([P, blocks, F2]),
                op=ADD,
            )
            if s % together == together - 1:
                rows = slice(piece * blocks * P, (piece + 1) * blocks * P)
                nc.sync.dma_start(
                    out=out[rows, s + 1 - together : s + 1, :].rearrange("(i p) a f -> p i (a f)", p=P),
                    in_=y_rows[:].rearrange("p i a f -> p i (a f)"),
                )

        def transpose_b1():
            turned = psum_acc.tile([P, 2, P], F32, tag="acc")
            for u in range(2):
                nc.tensor.transpose(turned[:, u, :], b1_rows[:].bitcast(F32)[:, u : F1 // 2 : 2], ident_f32[:])
            live["turned_b1"] = turned

        def keep_b1():
            nc.vector.tensor_copy(
                out=b1_words[:], in_=live["turned_b1"][:, :, 0:STYLES].rearrange("p u s -> p s u")
            )
            nc.vector.tensor_copy(
                out=b1_cols[:], in_=b1_words[:].rearrange("p s u -> p (s u)").bitcast(BF16)
            )

        def spread_b2():
            for half in range(2):
                spread = psum_y.tile([P, STYLES // 2, F2], BF16, name="y_acc")
                for a in range(STYLES // 2):
                    s = half * (STYLES // 2) + a
                    nc.tensor.matmul(
                        out=spread[:, a, :],
                        lhsT=ident_bf16[:, s : s + 1].to_broadcast([P, P]),
                        rhs=b2_rows[:],
                        start=True,
                        stop=True,
                    )
                nc.vector.tensor_copy(
                    out=b2_all[:, half * (STYLES // 2) : (half + 1) * (STYLES // 2), :], in_=spread[:]
                )

        def run(stage, s):
            if 0 <= s < STYLES:
                stage(s)

        def run_pieces(stage, s):
            if 0 <= s < STYLES:
                for piece in range(pieces(s)):
                    stage(s, piece)

        for n in range(-2, STYLES):
            run_pieces(group_h, n - 1)
            run_pieces(layer1_relu, n)
            run_pieces(layer2, n - 2)
            run(quantise_x, n + 1)
            if n == -1:
                sort_w1_scales(0)
                transpose_b1()
                keep_b1()
            if n == 0:
                spread_b2()
            run(transpose_x, n + 2)
            run(group_x, n + 2)
            run_pieces(quantise_h, n - 1)
            run_pieces(bias2_store, n - 2)
            if 0 < n + 2 < STYLES and (n + 2) % SHARE == 0:
                sort_w1_scales((n + 2) // SHARE)
            run(sort_w1, n + 2)

        last = STYLES - 1
        layer2(last - 1, 0)
        group_h(last, 0)
        bias2_store(last - 1, 0)
        for piece in range(LAST_PIECES):
            if piece > 0:
                group_h(last, piece)
            quantise_h(last, piece)
            layer2(last, piece)
        for piece in range(LAST_PIECES):
            bias2_store(last, piece)
